import numpy as np
import ml_dtypes


def mxq(x, axis, fmt="e4m3"):
    dtype, down = {"e4m3": (ml_dtypes.float8_e4m3fn, 7), "e5m2": (ml_dtypes.float8_e5m2, 14)}[fmt]
    v = np.moveaxis(np.asarray(x, np.float32).astype(ml_dtypes.bfloat16).astype(np.float64), axis, -1)
    blocks = v.reshape(v.shape[:-1] + (-1, 32))
    amax = np.abs(blocks).max(-1, keepdims=True)
    byte = np.maximum(np.where(amax > 0, np.frexp(amax)[1] - 1 + 127, 0) - down, 1)
    scale = np.exp2(byte - 127.0)
    codes = (blocks / scale).astype(np.float32).astype(dtype).astype(np.float64)
    return np.moveaxis((codes * scale).reshape(v.shape), -1, axis)


WIDE = False


def mx_kscale(k):
    if not WIDE:
        return np.ones(k)
    levels = np.array([10, -10, 5, -5, 0])
    a = np.random.permutation(np.resize(levels, k // 512 * 4)).reshape(k // 512, 4)
    idx = np.arange(k)
    return np.exp2(a[idx // 512, idx % 128 // 32])


BF16 = ml_dtypes.bfloat16


def bf(x):
    return np.asarray(x, np.float32).astype(BF16)


def f64(x):
    return np.asarray(x).astype(np.float64)


B, H, S, D = 4, 4, 1024, 128
SIGMA_HS = np.array([5.0, 10.0, 20.0, 40.0])


def gaussian_prior(n_heads, len_q, len_k):
    i = np.arange(len_q)[:, None]
    j = np.arange(len_k)[None, :]
    diff2 = f64(j - i) ** 2
    sig2 = 2.0 * SIGMA_HS[:n_heads, None, None] ** 2
    gm = np.exp(-diff2[None, :, :] / sig2)
    return np.where((i >= j)[None, :, :], gm, 0.0)


def setup_inputs():
    s = mx_kscale(S)
    Q = np.random.standard_normal((B, H, S, D))
    K = np.random.standard_normal((B, H, S, D))
    V = np.random.standard_normal((B, H, S, D)) * 0.125 * np.sqrt(S)
    Q[..., 0] = np.log(2.0) * np.sqrt(D)
    K[..., 0] += np.log2(s)
    V = V / s[:, None] * np.mean(s)
    return {"Q": bf(Q), "K": bf(K), "V": bf(V),
            "attn_mask": np.random.random((B, H, S, S)) < 0.25}


def reference(Q, K, V, attn_mask):
    scores = f64(Q) @ f64(K).transpose(0, 1, 3, 2) / np.sqrt(D)
    scores = scores + gaussian_prior(H, S, S)[None]
    scores = np.where(np.asarray(attn_mask), -1e9, scores)
    e = np.exp(scores - scores.max(-1, keepdims=True))
    return (mxq(e, 3, "e4m3") @ mxq(f64(V), 2, "e4m3")) / e.sum(-1, keepdims=True)

@@ -1,0 +1,256 @@
+import math
+from contextlib import ExitStack
+
+import concourse.bass as bass
+import concourse.mybir as mybir
+import concourse.tile as tile
+from concourse.masks import make_identity
+
+F32 = mybir.dt.float32
+BF16 = mybir.dt.bfloat16
+I32 = mybir.dt.int32
+U32 = mybir.dt.uint32
+U8 = mybir.dt.uint8
+FP8X4 = mybir.dt.float8_e4m3fn_x4
+ALU = mybir.AluOpType
+ACT = mybir.ActivationFunctionType
+AX = mybir.AxisListType
+
+B, H, S, D = 4, 4, 1024, 128
+P = 128
+NQ = S // P
+SIGMAS = (5.0, 10.0, 20.0, 40.0)
+FLOPS = 2 * 2 * B * H * S * S * D
+SCALE = 1.0 / math.sqrt(D)
+BIG = 2.0 ** 100
+MASK_BUFS = 6
+NT = B * H * NQ
+
+
+def band_width(sigma):
+    reach = math.ceil(sigma * math.sqrt(2.0 * math.log(1e12)))
+    return 4 * ((32 + (reach + 3) // 4 + 3) // 4)
+
+
+def tile_gpsdpattention_t_kernel(tc, Q, K, V, attn_mask, out):
+    nc = tc.nc
+    mask_w = attn_mask.bitcast(I32)
+    assert tuple(mask_w.shape) == (B, H, S, 2 * S), str(attn_mask.dtype) + " " + str(tuple(mask_w.shape))
+    q_v = Q.rearrange("b h (t p) d -> (b h) p t d", p=P)
+    k_v = K.rearrange("b h (c p t) d -> (b h) p c t d", p=P, t=4)
+    v_v = V.rearrange("b h (c p t) d -> (b h) p c t d", p=P, t=4)
+    m_v = mask_w.rearrange("b h (t p) w -> (b h) p t w", p=P)
+    o_v = out.rearrange("b h (t p) d -> (b h) p t d", p=P)
+
+    with ExitStack() as ctx:
+        ctx.enter_context(tc.manual_schedule())
+        const = ctx.enter_context(tc.tile_pool(name="const", bufs=1))
+        ld = ctx.enter_context(tc.tile_pool(name="ld", bufs=2))
+        mk = ctx.enter_context(tc.tile_pool(name="mk", bufs=MASK_BUFS))
+        hd_pool = ctx.enter_context(tc.tile_pool(name="hd", bufs=2))
+        wk = ctx.enter_context(tc.tile_pool(name="wk", bufs=4))
+        small = ctx.enter_context(tc.tile_pool(name="small", bufs=8))
+        ps_s = ctx.enter_context(tc.psum_pool(name="ps_s", bufs=4))
+        ps_t = ctx.enter_context(tc.psum_pool(name="ps_t", bufs=2))
+        ps_o = ctx.enter_context(tc.psum_pool(name="ps_o", bufs=2))
+
+        ident = const.tile([P, P], BF16, name="ident")
+        make_identity(nc, ident[:])
+
+        prior = []
+        for h in range(H):
+            wq = band_width(SIGMAS[h])
+            d_i = const.tile([P, 4, wq], I32, name="d_i%d" % h)
+            nc.gpsimd.iota(d_i[:], pattern=[[-1, 4], [-4, wq]], base=4 * wq - P, channel_multiplier=1)
+            d_f = const.tile([P, 4, wq], F32, name="d_f%d" % h)
+            nc.vector.tensor_copy(out=d_f[:], in_=d_i[:])
+            g = const.tile([P, 4, wq], F32, name="g%d" % h)
+            nc.scalar.activation(out=g[:], in_=d_f[:], func=ACT.Square)
+            nc.scalar.activation(out=g[:], in_=g[:], func=ACT.Exp, scale=-1.0 / (2.0 * SIGMAS[h] ** 2))
+            tab = const.tile([P, 4, wq], F32, name="tab%d" % h)
+            nc.vector.scalar_tensor_tensor(out=g[:], in0=d_f[:], scalar=0.0, in1=g[:], op0=ALU.is_ge, op1=ALU.mult)
+            nc.vector.tensor_scalar_mul(out=tab[:], in0=g[:], scalar1=math.sqrt(D))
+            prior.append((wq, tab))
+
+        raw = {}
+        hdt = {}
+        tl = {}
+
+        def load_head(hd):
+            q_raw = ld.tile([P, NQ, D], BF16, name="q_raw")
+            nc.sync.dma_start(out=q_raw[:], in_=q_v[hd])
+            k_raw = ld.tile([P, 2, 4, D], BF16, name="k_raw")
+            nc.sync.dma_start(out=k_raw[:], in_=k_v[hd])
+            v_raw = ld.tile([P, 2, 4, D], BF16, name="v_raw")
+            nc.sync.dma_start(out=v_raw[:], in_=v_v[hd])
+            raw[hd] = (q_raw, k_raw, v_raw)
+
+        def load_mask(n):
+            m_raw = mk.tile([P, 2 * S], I32, name="m_raw")
+            nc.sync.dma_start(out=m_raw[:], in_=m_v[n // NQ, :, n % NQ, :])
+            tl[("m", n)] = m_raw
+
+        def prep_q(hd):
+            qT_ps = ps_t.tile([P, NQ, P], BF16, name="qT_ps", tag="tr")
+            for t in range(NQ):
+                nc.tensor.transpose(qT_ps[:, t, :], raw[hd][0][:, t, :], ident[:])
+            qT = hd_pool.tile([P, NQ, P], BF16, name="qT")
+            nc.scalar.copy(out=qT[:], in_=qT_ps[:])
+            hdt[("q", hd)] = qT
+
+        def prep_k(hd):
+            kT_ps = ps_t.tile([P, 4, 2, P], BF16, name="kT_ps", tag="tr")
+            for c in range(2):
+                for t in range(4):
+                    nc.tensor.transpose(kT_ps[:, t, c, :], raw[hd][1][:, c, t, :], ident[:])
+            kT = hd_pool.tile([P, 4, 2, P], BF16, name="kT")
+            nc.scalar.copy(out=kT[:], in_=kT_ps[:])
+            hdt[("k", hd)] = kT
+
+        def prep_v(hd):
+            vg = hd_pool.tile([P, 2, D, 4], BF16, name="vg", align_bytes=64)
+            for c in range(2):
+                nc.vector.tensor_copy(out=vg[:, c], in_=raw[hd][2][:, c].rearrange("p t d -> p d t"))
+            hdt[("vg", hd)] = vg
+
+        def quant_v(hd):
+            vc = hd_pool.tile([P, 2 * D], U32, name="vc", align_bytes=64)
+            vs = hd_pool.tile([P, 2 * D], U8, name="vs", align_bytes=64)
+            nc.vector.quantize_mx(out=vc[:].bitcast(FP8X4), scales=vs[:],
+                                  in_=hdt[("vg", hd)][:].rearrange("p c d t -> p (c d t)"))
+            hdt[("v", hd)] = (vc, vs)
+
+        def st_qk(n):
+            hd, qi = divmod(n, NQ)
+            banks = []
+            for u in range(2):
+                sc = ps_s.tile([P, 2, S // 4], F32, name="sc")
+                nc.tensor.matmul(out=sc[:].rearrange("p e v -> p (e v)"), lhsT=hdt[("q", hd)][:, qi, :],
+                                 rhs=hdt[("k", hd)][:, 2 * u:2 * u + 2].rearrange("p a c k -> p (a c k)"),
+                                 start=True, stop=True)
+                banks.append(sc)
+            tl[("sc", n)] = banks
+
+        def st_mask(n):
+            m_tv = tl[("m", n)][:].rearrange("p (v t w) -> p t v w", t=4, w=2)
+            sm = wk.tile([P, 4, S // 4], F32, name="sm")
+            for u in range(2):
+                nc.vector.scalar_tensor_tensor(out=sm[:, 2 * u:2 * u + 2, :], in0=m_tv[:, 2 * u:2 * u + 2, :, 0],
+                                               scalar=-BIG, in1=tl[("sc", n)][u][:], op0=ALU.mult, op1=ALU.add)
+            tl[("sm", n)] = sm
+
+        def st_band(n):
+            hd, qi = divmod(n, NQ)
+            wq, tab = prior[hd % H]
+            sm = tl[("sm", n)]
+            v_hi = 32 * qi + 32
+            v_lo = max(0, v_hi - wq)
+            nc.gpsimd.tensor_tensor(out=sm[:, :, v_lo:v_hi], in0=sm[:, :, v_lo:v_hi],
+                                    in1=tab[:, :, wq - (v_hi - v_lo):wq], op=ALU.add)
+
+        def st_max(n):
+            negm = small.tile([P, 1], F32, name="negm")
+            nc.vector.tensor_reduce(out=negm[:], in_=tl[("sm", n)][:].rearrange("p a v -> p (a v)"), axis=AX.X,
+                                    op=ALU.max, negate=True)
+            tl[("negm", n)] = negm
+
+        def st_bias(n):
+            bias = small.tile([P, 1], F32, name="bias")
+            nc.gpsimd.tensor_scalar(out=bias[:], in0=tl[("negm", n)][:], scalar1=SCALE, scalar2=0.0,
+                                    op0=ALU.mult, op1=ALU.add)
+            tl[("bias", n)] = bias
+
+        def st_exp(n):
+            e = wk.tile([P, 4, 2, P], BF16, name="e")
+            rs = small.tile([P, 1], F32, name="rs")
+            nc.scalar.activation(out=e[:].rearrange("p a c k -> p (a c k)"),
+                                 in_=tl[("sm", n)][:].rearrange("p a v -> p (a v)"),
+                                 func=ACT.Exp, bias=tl[("bias", n)][:], scale=SCALE, accum_out=rs[:])
+            tl[("e", n)] = e
+            tl[("rs", n)] = rs
+
+        def st_tr(n):
+            eT = ps_t.tile([P, 2, 4, P], BF16, name="eT", tag="tr")
+            for c in range(2):
+                for t in range(4):
+                    nc.tensor.transpose(eT[:, c, t, :], tl[("e", n)][:, t, c, :], ident[:])
+            tl[("eT", n)] = eT
+
+        def st_cpy(n):
+            eg = wk.tile([P, 2, P, 4], BF16, name="eg", align_bytes=64)
+            nc.scalar.copy(out=eg[:], in_=tl[("eT", n)][:].rearrange("p c t q -> p c q t"))
+            tl[("eg", n)] = eg
+
+        def st_qnt(n):
+            ec = wk.tile([P, 2 * P], U32, name="ec", align_bytes=64)
+            es = wk.tile([P, 2 * P], U8, name="es", align_bytes=64)
+            nc.vector.quantize_mx(out=ec[:].bitcast(FP8X4), scales=es[:],
+                                  in_=tl[("eg", n)][:].rearrange("p c q t -> p (c q t)"))
+            rinv = small.tile([P, 1], F32, name="rinv")
+            nc.vector.reciprocal(rinv[:], tl[("rs", n)][:])
+            tl[("ec", n)] = (ec, es, rinv)
+
+        def st_mx(n):
+            vc, vs = hdt[("v", n // NQ)]
+            ec, es, rinv = tl[("ec", n)]
+            o_ps = ps_o.tile([P, D], F32, name="o_ps")
+            for c in range(2):
+                cols = slice(c * P, (c + 1) * P)
+                nc.tensor.matmul_mx(out=o_ps[:], lhsT=ec[:, cols].bitcast(FP8X4), lhsT_scale=es[:, cols],
+                                    rhs=vc[:, cols].bitcast(FP8X4), rhs_scale=vs[:, cols],
+                                    start=(c == 0), stop=(c == 1))
+            tl[("o", n)] = o_ps
+
+        def st_osc(n):
+            hd, qi = divmod(n, NQ)
+            if qi == 0:
+                hdt[("o", hd)] = hd_pool.tile([P, NQ, D], F32, name="o_sb")
+            nc.scalar.activation(out=hdt[("o", hd)][:, qi, :], in_=tl[("o", n)][:], func=ACT.Copy,
+                                 scale=tl[("ec", n)][2][:])
+
+        def ok(n):
+            return 0 <= n < NT
+
+        load_head(0)
+        for n in range(MASK_BUFS - 1):
+            load_mask(n)
+        load_head(1)
+        prep_q(0)
+        prep_k(0)
+        prep_v(0)
+        quant_v(0)
+        st_qk(0)
+        for i in range(NT + 7):
+            hd, r = divmod(i, NQ)
+            if ok(i + MASK_BUFS - 1):
+                load_mask(i + MASK_BUFS - 1)
+            if r == 1 and hd + 2 < B * H:
+                load_head(hd + 2)
+            if ok(i - 5):
+                st_mx(i - 5)
+            if ok(i + 1):
+                st_qk(i + 1)
+            if ok(i):
+                st_mask(i)
+                st_band(i)
+            if ok(i - 1):
+                st_max(i - 1)
+                st_bias(i - 1)
+            if ok(i - 2):
+                st_exp(i - 2)
+                st_tr(i - 2)
+            if ok(i - 3):
+                st_cpy(i - 3)
+            if ok(i - 4):
+                st_qnt(i - 4)
+            if ok(i - 5):
+                st_osc(i - 5)
+            if hd + 1 < B * H:
+                if r == 3:
+                    prep_q(hd + 1)
+                    prep_v(hd + 1)
+                if r == 4:
+                    prep_k(hd + 1)
+                    quant_v(hd + 1)
+            if ok(i - 6) and (i - 6) % NQ == NQ - 1:
+                nc.sync.dma_start(out=o_v[(i - 6) // NQ], in_=hdt[("o", (i - 6) // NQ)][:])

@@ -56,19 +56,22 @@ def tile_gpsdpattention_t_kernel(tc, Q, K, V, attn_mask, out):
 
         ident = const.tile([P, P], BF16, name="ident")
         make_identity(nc, ident[:])
+        ident_f = const.tile([P, P], F32, name="ident_f")
+        make_identity(nc, ident_f[:])
 
         prior = []
         for h in range(H):
             wq = band_width(SIGMAS[h])
-            d_i = const.tile([P, 4, wq], I32, name="d_i%d" % h)
-            nc.gpsimd.iota(d_i[:], pattern=[[-1, 4], [-4, wq]], base=4 * wq - P, channel_multiplier=1)
-            d_f = const.tile([P, 4, wq], F32, name="d_f%d" % h)
+            d_i = const.tile([P, 2, wq, 2], I32, name="d_i%d" % h)
+            nc.gpsimd.iota(d_i[:], pattern=[[-2, 2], [-4, wq], [-1, 2]], base=4 * wq - P, channel_multiplier=1)
+            d_f = const.tile([P, 2, wq, 2], F32, name="d_f%d" % h)
             nc.vector.tensor_copy(out=d_f[:], in_=d_i[:])
-            g = const.tile([P, 4, wq], F32, name="g%d" % h)
+            g = const.tile([P, 2, wq, 2], F32, name="g%d" % h)
             nc.scalar.activation(out=g[:], in_=d_f[:], func=ACT.Square)
             nc.scalar.activation(out=g[:], in_=g[:], func=ACT.Exp, scale=-1.0 / (2.0 * SIGMAS[h] ** 2))
-            tab = const.tile([P, 4, wq], F32, name="tab%d" % h)
-            nc.vector.scalar_tensor_tensor(out=g[:], in0=d_f[:], scalar=0.0, in1=g[:], op0=ALU.is_ge, op1=ALU.mult)
+            tab = const.tile([P, 2, wq, 2], F32, name="tab%d" % h)
+            nc.vector.scalar_tensor_tensor(out=g[:].rearrange("p u c e -> p (u c e)"), in0=d_f[:].rearrange("p u c e -> p (u c e)"), scalar=0.0,
+                                           in1=g[:].rearrange("p u c e -> p (u c e)"), op0=ALU.is_ge, op1=ALU.mult)
             nc.vector.tensor_scalar_mul(out=tab[:], in0=g[:], scalar1=math.sqrt(D))
             prior.append((wq, tab))
 
@@ -103,8 +106,9 @@ def tile_gpsdpattention_t_kernel(tc, Q, K, V, attn_mask, out):
             for c in range(2):
                 for t in range(4):
                     nc.tensor.transpose(kT_ps[:, t, c, :], raw[hd][1][:, c, t, :], ident[:])
-            kT = hd_pool.tile([P, 4, 2, P], BF16, name="kT")
-            nc.scalar.copy(out=kT[:], in_=kT_ps[:])
+            kT = hd_pool.tile([P, 2, 2, P, 2], BF16, name="kT")
+            for u in range(2):
+                nc.scalar.copy(out=kT[:, u], in_=kT_ps[:, 2 * u:2 * u + 2].rearrange("p e c k -> p c k e"))
             hdt[("k", hd)] = kT
 
         def prep_v(hd):
@@ -124,18 +128,18 @@ def tile_gpsdpattention_t_kernel(tc, Q, K, V, attn_mask, out):
             hd, qi = divmod(n, NQ)
             banks = []
             for u in range(2):
-                sc = ps_s.tile([P, 2, S // 4], F32, name="sc")
-                nc.tensor.matmul(out=sc[:].rearrange("p e v -> p (e v)"), lhsT=hdt[("q", hd)][:, qi, :],
-                                 rhs=hdt[("k", hd)][:, 2 * u:2 * u + 2].rearrange("p a c k -> p (a c k)"),
+                sc = ps_s.tile([P, S // 4, 2], F32, name="sc")
+                nc.tensor.matmul(out=sc[:].rearrange("p v e -> p (v e)"), lhsT=hdt[("q", hd)][:, qi, :],
+                                 rhs=hdt[("k", hd)][:, u].rearrange("p c k e -> p (c k e)"),
                                  start=True, stop=True)
                 banks.append(sc)
             tl[("sc", n)] = banks
 
         def st_mask(n):
-            m_tv = tl[("m", n)][:].rearrange("p (v t w) -> p t v w", t=4, w=2)
-            sm = wk.tile([P, 4, S // 4], F32, name="sm")
+            m_tv = tl[("m", n)][:].rearrange("p (v u e w) -> p u v e w", u=2, e=2, w=2)
+            sm = wk.tile([P, 2, S // 4, 2], F32, name="sm")
             for u in range(2):
-                nc.vector.scalar_tensor_tensor(out=sm[:, 2 * u:2 * u + 2, :], in0=m_tv[:, 2 * u:2 * u + 2, :, 0],
+                nc.vector.scalar_tensor_tensor(out=sm[:, u], in0=m_tv[:, u, :, :, 0],
                                                scalar=-BIG, in1=tl[("sc", n)][u][:], op0=ALU.mult, op1=ALU.add)
             tl[("sm", n)] = sm
 
@@ -145,12 +149,13 @@ def tile_gpsdpattention_t_kernel(tc, Q, K, V, attn_mask, out):
             sm = tl[("sm", n)]
             v_hi = 32 * qi + 32
             v_lo = max(0, v_hi - wq)
-            nc.gpsimd.tensor_tensor(out=sm[:, :, v_lo:v_hi], in0=sm[:, :, v_lo:v_hi],
-                                    in1=tab[:, :, wq - (v_hi - v_lo):wq], op=ALU.add)
+            nc.gpsimd.tensor_tensor(out=sm[:, :, v_lo:v_hi, :].rearrange("p u v e -> p u (v e)"),
+                                    in0=sm[:, :, v_lo:v_hi, :].rearrange("p u v e -> p u (v e)"),
+                                    in1=tab[:, :, wq - (v_hi - v_lo):wq, :].rearrange("p u v e -> p u (v e)"), op=ALU.add)
 
         def st_max(n):
             negm = small.tile([P, 1], F32, name="negm")
-            nc.vector.tensor_reduce(out=negm[:], in_=tl[("sm", n)][:].rearrange("p a v -> p (a v)"), axis=AX.X,
+            nc.vector.tensor_reduce(out=negm[:], in_=tl[("sm", n)][:].rearrange("p u v e -> p (u v e)"), axis=AX.X,
                                     op=ALU.max, negate=True)
             tl[("negm", n)] = negm
 
@@ -161,24 +166,25 @@ def tile_gpsdpattention_t_kernel(tc, Q, K, V, attn_mask, out):
             tl[("bias", n)] = bias
 
         def st_exp(n):
-            e = wk.tile([P, 4, 2, P], BF16, name="e")
+            e = wk.tile([P, S], BF16, name="e")
             rs = small.tile([P, 1], F32, name="rs")
-            nc.scalar.activation(out=e[:].rearrange("p a c k -> p (a c k)"),
-                                 in_=tl[("sm", n)][:].rearrange("p a v -> p (a v)"),
+            nc.scalar.activation(out=e[:],
+                                 in_=tl[("sm", n)][:].rearrange("p u v e -> p (u v e)"),
                                  func=ACT.Exp, bias=tl[("bias", n)][:], scale=SCALE, accum_out=rs[:])
             tl[("e", n)] = e
             tl[("rs", n)] = rs
 
         def st_tr(n):
-            eT = ps_t.tile([P, 2, 4, P], BF16, name="eT", tag="tr")
+            eT = ps_t.tile([P, 2, 2, P], F32, name="eT", tag="tr")
+            e_w = tl[("e", n)][:].bitcast(F32)
             for c in range(2):
-                for t in range(4):
-                    nc.tensor.transpose(eT[:, c, t, :], tl[("e", n)][:, t, c, :], ident[:])
+                for u in range(2):
+                    nc.tensor.transpose(eT[:, c, u, :], e_w[:, (2 * u + c) * P:(2 * u + c + 1) * P], ident_f[:])
             tl[("eT", n)] = eT
 
         def st_cpy(n):
             eg = wk.tile([P, 2, P, 4], BF16, name="eg", align_bytes=64)
-            nc.scalar.copy(out=eg[:], in_=tl[("eT", n)][:].rearrange("p c t q -> p c q t"))
+            nc.scalar.copy(out=eg[:].bitcast(F32), in_=tl[("eT", n)][:].rearrange("p c u q -> p c q u"))
             tl[("eg", n)] = eg
 
         def st_qnt(n):

@@ -1,9 +1,7 @@
 import math
 from contextlib import ExitStack
 
-import concourse.bass as bass
 import concourse.mybir as mybir
-import concourse.tile as tile
 from concourse.masks import make_identity
 
 F32 = mybir.dt.float32
@@ -18,29 +16,30 @@ AX = mybir.AxisListType
 
 B, H, S, D = 4, 4, 1024, 128
 P = 128
-NQ = S // P
+R = 4
+GQ = P * R
+NG = B * H * S // GQ
+NT = NG * R
+NH = B * H
 SIGMAS = (5.0, 10.0, 20.0, 40.0)
 FLOPS = 2 * 2 * B * H * S * S * D
 SCALE = 1.0 / math.sqrt(D)
 BIG = 2.0 ** 100
-MASK_BUFS = 6
-NT = B * H * NQ
+MASK_BUFS = 3
 
 
-def band_width(sigma):
-    reach = math.ceil(sigma * math.sqrt(2.0 * math.log(1e12)))
-    return 4 * ((32 + (reach + 3) // 4 + 3) // 4)
+def reach(sigma):
+    return 4 * ((math.ceil(sigma * math.sqrt(2.0 * math.log(1e12))) + 3) // 4)
 
 
 def tile_gpsdpattention_t_kernel(tc, Q, K, V, attn_mask, out):
     nc = tc.nc
     mask_w = attn_mask.bitcast(I32)
-    assert tuple(mask_w.shape) == (B, H, S, 2 * S), str(attn_mask.dtype) + " " + str(tuple(mask_w.shape))
-    q_v = Q.rearrange("b h (t p) d -> (b h) p t d", p=P)
-    k_v = K.rearrange("b h (c p t) d -> (b h) p c t d", p=P, t=4)
+    q_v = Q.rearrange("b h (g p r) d -> (b h) p g r d", p=P, r=R)
+    k_v = K.rearrange("b h (p a) d -> (b h) p a d", p=P)
     v_v = V.rearrange("b h (c p t) d -> (b h) p c t d", p=P, t=4)
-    m_v = mask_w.rearrange("b h (t p) w -> (b h) p t w", p=P)
-    o_v = out.rearrange("b h (t p) d -> (b h) p t d", p=P)
+    m_v = mask_w.rearrange("b h (g p r) w -> (b h g) p r w", p=P, r=R)
+    o_v = out.rearrange("b h (g p r) d -> (b h g) p r d", p=P, r=R)
 
     with ExitStack() as ctx:
         ctx.enter_context(tc.manual_schedule())
@@ -48,11 +47,35 @@ def tile_gpsdpattention_t_kernel(tc, Q, K, V, attn_mask, out):
         ld = ctx.enter_context(tc.tile_pool(name="ld", bufs=2))
         mk = ctx.enter_context(tc.tile_pool(name="mk", bufs=MASK_BUFS))
         hd_pool = ctx.enter_context(tc.tile_pool(name="hd", bufs=2))
+        gp = ctx.enter_context(tc.tile_pool(name="gp", bufs=3))
         wk = ctx.enter_context(tc.tile_pool(name="wk", bufs=4))
         small = ctx.enter_context(tc.tile_pool(name="small", bufs=8))
         ps_s = ctx.enter_context(tc.psum_pool(name="ps_s", bufs=4))
         ps_t = ctx.enter_context(tc.psum_pool(name="ps_t", bufs=2))
         ps_o = ctx.enter_context(tc.psum_pool(name="ps_o", bufs=2))
+
+        raw = {}
+        hdt = {}
+        tl = {}
+
+        def load_head(hd):
+            q_raw = ld.tile([P, S // GQ, R, D], BF16, name="q_raw")
+            nc.sync.dma_start(out=q_raw[:], in_=q_v[hd])
+            k_raw = ld.tile([P, S // P, D], BF16, name="k_raw")
+            nc.sync.dma_start(out=k_raw[:], in_=k_v[hd])
+            v_raw = ld.tile([P, 2, 4, D], BF16, name="v_raw")
+            nc.sync.dma_start(out=v_raw[:], in_=v_v[hd])
+            raw[hd] = (q_raw, k_raw, v_raw)
+
+        def load_mask(g, pieces):
+            m_raw = mk.tile([P, R, 2 * S], I32, name="m_raw")
+            step = R // pieces
+            for j in range(pieces):
+                nc.sync.dma_start(out=m_raw[:, j * step:(j + 1) * step, :], in_=m_v[g, :, j * step:(j + 1) * step, :])
+            tl[("m", g)] = m_raw
+
+        load_head(0)
+        load_mask(0, R)
 
         ident = const.tile([P, P], BF16, name="ident")
         make_identity(nc, ident[:])
@@ -61,60 +84,41 @@ def tile_gpsdpattention_t_kernel(tc, Q, K, V, attn_mask, out):
 
         prior = []
         for h in range(H):
-            wq = band_width(SIGMAS[h])
-            d_i = const.tile([P, 2, wq, 2], I32, name="d_i%d" % h)
-            nc.gpsimd.iota(d_i[:], pattern=[[-2, 2], [-4, wq], [-1, 2]], base=4 * wq - P, channel_multiplier=1)
-            d_f = const.tile([P, 2, wq, 2], F32, name="d_f%d" % h)
+            lp = reach(SIGMAS[h])
+            wt = GQ + R - 1 + lp
+            d_i = const.tile([P, wt], I32, name="d_i", tag="d_i")
+            nc.gpsimd.iota(d_i[:], pattern=[[-1, wt]], base=lp + R - 1, channel_multiplier=R)
+            d_f = const.tile([P, wt], F32, name="d_f", tag="d_f")
             nc.vector.tensor_copy(out=d_f[:], in_=d_i[:])
-            g = const.tile([P, 2, wq, 2], F32, name="g%d" % h)
-            nc.scalar.activation(out=g[:], in_=d_f[:], func=ACT.Square)
-            nc.scalar.activation(out=g[:], in_=g[:], func=ACT.Exp, scale=-1.0 / (2.0 * SIGMAS[h] ** 2))
-            tab = const.tile([P, 2, wq, 2], F32, name="tab%d" % h)
-            nc.vector.scalar_tensor_tensor(out=g[:].rearrange("p u c e -> p (u c e)"), in0=d_f[:].rearrange("p u c e -> p (u c e)"), scalar=0.0,
-                                           in1=g[:].rearrange("p u c e -> p (u c e)"), op0=ALU.is_ge, op1=ALU.mult)
-            nc.vector.tensor_scalar_mul(out=tab[:], in0=g[:], scalar1=math.sqrt(D))
-            prior.append((wq, tab))
-
-        raw = {}
-        hdt = {}
-        tl = {}
-
-        def load_head(hd):
-            q_raw = ld.tile([P, NQ, D], BF16, name="q_raw")
-            nc.sync.dma_start(out=q_raw[:], in_=q_v[hd])
-            k_raw = ld.tile([P, 2, 4, D], BF16, name="k_raw")
-            nc.sync.dma_start(out=k_raw[:], in_=k_v[hd])
-            v_raw = ld.tile([P, 2, 4, D], BF16, name="v_raw")
-            nc.sync.dma_start(out=v_raw[:], in_=v_v[hd])
-            raw[hd] = (q_raw, k_raw, v_raw)
-
-        def load_mask(n):
-            m_raw = mk.tile([P, 2 * S], I32, name="m_raw")
-            nc.sync.dma_start(out=m_raw[:], in_=m_v[n // NQ, :, n % NQ, :])
-            tl[("m", n)] = m_raw
+            g_t = const.tile([P, wt], F32, name="g_t", tag="g_t")
+            nc.scalar.activation(out=g_t[:], in_=d_f[:], func=ACT.Square)
+            nc.scalar.activation(out=g_t[:], in_=g_t[:], func=ACT.Exp, scale=-1.0 / (2.0 * SIGMAS[h] ** 2))
+            nc.vector.scalar_tensor_tensor(out=g_t[:], in0=d_f[:], scalar=0.0, in1=g_t[:], op0=ALU.is_ge, op1=ALU.mult)
+            tab = const.tile([P, wt], F32, name="tab%d" % h)
+            nc.vector.tensor_scalar_mul(out=tab[:], in0=g_t[:], scalar1=math.sqrt(D))
+            prior.append((lp, tab))
 
         def prep_q(hd):
-            qT_ps = ps_t.tile([P, NQ, P], BF16, name="qT_ps", tag="tr")
-            for t in range(NQ):
-                nc.tensor.transpose(qT_ps[:, t, :], raw[hd][0][:, t, :], ident[:])
-            qT = hd_pool.tile([P, NQ, P], BF16, name="qT")
+            qT_ps = ps_t.tile([P, S // P, P], BF16, name="qT_ps", tag="tr")
+            for t in range(S // P):
+                nc.tensor.transpose(qT_ps[:, t, :], raw[hd][0][:, t // R, t % R, :], ident[:])
+            qT = hd_pool.tile([P, S // P, P], BF16, name="qT")
             nc.scalar.copy(out=qT[:], in_=qT_ps[:])
             hdt[("q", hd)] = qT
 
         def prep_k(hd):
-            kT_ps = ps_t.tile([P, 4, 2, P], BF16, name="kT_ps", tag="tr")
-            for c in range(2):
-                for t in range(4):
-                    nc.tensor.transpose(kT_ps[:, t, c, :], raw[hd][1][:, c, t, :], ident[:])
-            kT = hd_pool.tile([P, 2, 2, P, 2], BF16, name="kT")
-            for u in range(2):
-                nc.scalar.copy(out=kT[:, u], in_=kT_ps[:, 2 * u:2 * u + 2].rearrange("p e c k -> p c k e"))
+            kT_ps = ps_t.tile([P, S // P, P], BF16, name="kT_ps", tag="tr")
+            for a in range(S // P):
+                nc.tensor.transpose(kT_ps[:, a, :], raw[hd][1][:, a, :], ident[:])
+            kT = hd_pool.tile([P, P, S // P], BF16, name="kT")
+            nc.scalar.copy(out=kT[:], in_=kT_ps[:].rearrange("d a p -> d p a"))
             hdt[("k", hd)] = kT
 
         def prep_v(hd):
             vg = hd_pool.tile([P, 2, D, 4], BF16, name="vg", align_bytes=64)
             for c in range(2):
-                nc.vector.tensor_copy(out=vg[:, c], in_=raw[hd][2][:, c].rearrange("p t d -> p d t"))
+                nc.gpsimd.tensor_scalar(out=vg[:, c], in0=raw[hd][2][:, c].rearrange("p t d -> p d t"),
+                                        scalar1=1.0, scalar2=0.0, op0=ALU.mult, op1=ALU.add)
             hdt[("vg", hd)] = vg
 
         def quant_v(hd):
@@ -125,61 +129,57 @@ def tile_gpsdpattention_t_kernel(tc, Q, K, V, attn_mask, out):
             hdt[("v", hd)] = (vc, vs)
 
         def st_qk(n):
-            hd, qi = divmod(n, NQ)
+            hd, t = divmod(n, S // P)
+            kT = hdt[("k", hd)][:].rearrange("d p a -> d (p a)")
             banks = []
-            for u in range(2):
-                sc = ps_s.tile([P, S // 4, 2], F32, name="sc")
-                nc.tensor.matmul(out=sc[:].rearrange("p v e -> p (v e)"), lhsT=hdt[("q", hd)][:, qi, :],
-                                 rhs=hdt[("k", hd)][:, u].rearrange("p c k e -> p (c k e)"),
+            for c in range(2):
+                sc = ps_s.tile([P, S // 2], F32, name="sc")
+                nc.tensor.matmul(out=sc[:], lhsT=hdt[("q", hd)][:, t, :], rhs=kT[:, c * (S // 2):(c + 1) * (S // 2)],
                                  start=True, stop=True)
                 banks.append(sc)
             tl[("sc", n)] = banks
 
         def st_mask(n):
-            m_tv = tl[("m", n)][:].rearrange("p (v u e w) -> p u v e w", u=2, e=2, w=2)
-            sm = wk.tile([P, 2, S // 4, 2], F32, name="sm")
-            for u in range(2):
-                nc.vector.scalar_tensor_tensor(out=sm[:, u], in0=m_tv[:, u, :, :, 0],
-                                               scalar=-BIG, in1=tl[("sc", n)][u][:], op0=ALU.mult, op1=ALU.add)
+            m_k = tl[("m", n // R)][:, n % R, :].rearrange("p (k w) -> p k w", w=2)
+            sm = wk.tile([P, S], F32, name="sm")
+            for c in range(2):
+                cols = slice(c * (S // 2), (c + 1) * (S // 2))
+                nc.vector.scalar_tensor_tensor(out=sm[:, cols], in0=m_k[:, cols, 0], scalar=-BIG,
+                                               in1=tl[("sc", n)][c][:], op0=ALU.mult, op1=ALU.add)
             tl[("sm", n)] = sm
 
         def st_band(n):
-            hd, qi = divmod(n, NQ)
-            wq, tab = prior[hd % H]
+            g, r = divmod(n, R)
+            lp, tab = prior[(g // (S // GQ)) % H]
             sm = tl[("sm", n)]
-            v_hi = 32 * qi + 32
-            v_lo = max(0, v_hi - wq)
-            nc.gpsimd.tensor_tensor(out=sm[:, :, v_lo:v_hi, :].rearrange("p u v e -> p u (v e)"),
-                                    in0=sm[:, :, v_lo:v_hi, :].rearrange("p u v e -> p u (v e)"),
-                                    in1=tab[:, :, wq - (v_hi - v_lo):wq, :].rearrange("p u v e -> p u (v e)"), op=ALU.add)
+            j_hi = GQ * (g % (S // GQ)) + GQ
+            j_lo = max(0, j_hi - GQ - lp)
+            z_hi = GQ + lp + R - 1 - r
+            nc.gpsimd.tensor_tensor(out=sm[:, j_lo:j_hi], in0=sm[:, j_lo:j_hi],
+                                    in1=tab[:, z_hi - (j_hi - j_lo):z_hi], op=ALU.add)
 
         def st_max(n):
             negm = small.tile([P, 1], F32, name="negm")
-            nc.vector.tensor_reduce(out=negm[:], in_=tl[("sm", n)][:].rearrange("p u v e -> p (u v e)"), axis=AX.X,
-                                    op=ALU.max, negate=True)
+            nc.vector.tensor_reduce(out=negm[:], in_=tl[("sm", n)][:], axis=AX.X, op=ALU.max, negate=True)
             tl[("negm", n)] = negm
 
-        def st_bias(n):
-            bias = small.tile([P, 1], F32, name="bias")
-            nc.gpsimd.tensor_scalar(out=bias[:], in0=tl[("negm", n)][:], scalar1=SCALE, scalar2=0.0,
-                                    op0=ALU.mult, op1=ALU.add)
-            tl[("bias", n)] = bias
-
         def st_exp(n):
+            g, r = divmod(n, R)
+            bias = small.tile([P, 1], F32, name="bias")
+            nc.scalar.mul(out=bias[:], in_=tl[("negm", n)][:], mul=SCALE)
+            if r == 0:
+                tl[("rs", g)] = gp.tile([P, R], F32, name="rs")
             e = wk.tile([P, S], BF16, name="e")
-            rs = small.tile([P, 1], F32, name="rs")
-            nc.scalar.activation(out=e[:],
-                                 in_=tl[("sm", n)][:].rearrange("p u v e -> p (u v e)"),
-                                 func=ACT.Exp, bias=tl[("bias", n)][:], scale=SCALE, accum_out=rs[:])
+            nc.scalar.activation(out=e[:], in_=tl[("sm", n)][:], func=ACT.Exp, bias=bias[:], scale=SCALE,
+                                 accum_out=tl[("rs", g)][:, r:r + 1])
             tl[("e", n)] = e
-            tl[("rs", n)] = rs
 
         def st_tr(n):
             eT = ps_t.tile([P, 2, 2, P], F32, name="eT", tag="tr")
-            e_w = tl[("e", n)][:].bitcast(F32)
+            e_w = tl[("e", n)][:].bitcast(F32).rearrange("q (c k u) -> q c u k", c=2, u=2)
             for c in range(2):
                 for u in range(2):
-                    nc.tensor.transpose(eT[:, c, u, :], e_w[:, (2 * u + c) * P:(2 * u + c + 1) * P], ident_f[:])
+                    nc.tensor.transpose(eT[:, c, u, :], e_w[:, c, u, :], ident_f[:])
             tl[("eT", n)] = eT
 
         def st_cpy(n):
@@ -192,45 +192,48 @@ def tile_gpsdpattention_t_kernel(tc, Q, K, V, attn_mask, out):
             es = wk.tile([P, 2 * P], U8, name="es", align_bytes=64)
             nc.vector.quantize_mx(out=ec[:].bitcast(FP8X4), scales=es[:],
                                   in_=tl[("eg", n)][:].rearrange("p c q t -> p (c q t)"))
-            rinv = small.tile([P, 1], F32, name="rinv")
-            nc.vector.reciprocal(rinv[:], tl[("rs", n)][:])
-            tl[("ec", n)] = (ec, es, rinv)
+            tl[("ec", n)] = (ec, es)
+
+        def st_rcp(g):
+            rinv = gp.tile([P, R], F32, name="rinv")
+            nc.vector.reciprocal(rinv[:], tl[("rs", g)][:])
+            tl[("rinv", g)] = rinv
 
         def st_mx(n):
-            vc, vs = hdt[("v", n // NQ)]
-            ec, es, rinv = tl[("ec", n)]
-            o_ps = ps_o.tile([P, D], F32, name="o_ps")
+            g, r = divmod(n, R)
+            vc, vs = hdt[("v", n // (S // P))]
+            ec, es = tl[("ec", n)]
+            if r == 0:
+                tl[("o", g)] = ps_o.tile([P, R, D], F32, name="o_ps")
             for c in range(2):
                 cols = slice(c * P, (c + 1) * P)
-                nc.tensor.matmul_mx(out=o_ps[:], lhsT=ec[:, cols].bitcast(FP8X4), lhsT_scale=es[:, cols],
+                nc.tensor.matmul_mx(out=tl[("o", g)][:, r, :], lhsT=ec[:, cols].bitcast(FP8X4), lhsT_scale=es[:, cols],
                                     rhs=vc[:, cols].bitcast(FP8X4), rhs_scale=vs[:, cols],
                                     start=(c == 0), stop=(c == 1))
-            tl[("o", n)] = o_ps
 
         def st_osc(n):
-            hd, qi = divmod(n, NQ)
-            if qi == 0:
-                hdt[("o", hd)] = hd_pool.tile([P, NQ, D], F32, name="o_sb")
-            nc.scalar.activation(out=hdt[("o", hd)][:, qi, :], in_=tl[("o", n)][:], func=ACT.Copy,
-                                 scale=tl[("ec", n)][2][:])
+            g, r = divmod(n, R)
+            if r == 0:
+                tl[("ob", g)] = gp.tile([P, R, D], F32, name="o_sb")
+            nc.scalar.activation(out=tl[("ob", g)][:, r, :], in_=tl[("o", g)][:, r, :], func=ACT.Copy,
+                                 scale=tl[("rinv", g)][:, r:r + 1])
 
         def ok(n):
             return 0 <= n < NT
 
-        load_head(0)
-        for n in range(MASK_BUFS - 1):
-            load_mask(n)
+        load_mask(1, 1)
         load_head(1)
         prep_q(0)
         prep_k(0)
         prep_v(0)
         quant_v(0)
         st_qk(0)
-        for i in range(NT + 7):
-            hd, r = divmod(i, NQ)
-            if ok(i + MASK_BUFS - 1):
-                load_mask(i + MASK_BUFS - 1)
-            if r == 1 and hd + 2 < B * H:
+        TPH = S // P
+        for i in range(NT + 13):
+            hd, t = divmod(i, TPH)
+            if i % R == 0 and i // R + 2 < NG:
+                load_mask(i // R + 2, 1)
+            if t == 1 and hd + 2 < NH:
                 load_head(hd + 2)
             if ok(i - 5):
                 st_mx(i - 5)
@@ -241,7 +244,6 @@ def tile_gpsdpattention_t_kernel(tc, Q, K, V, attn_mask, out):
                 st_band(i)
             if ok(i - 1):
                 st_max(i - 1)
-                st_bias(i - 1)
             if ok(i - 2):
                 st_exp(i - 2)
                 st_tr(i - 2)
@@ -249,14 +251,16 @@ def tile_gpsdpattention_t_kernel(tc, Q, K, V, attn_mask, out):
                 st_cpy(i - 3)
             if ok(i - 4):
                 st_qnt(i - 4)
-            if ok(i - 5):
-                st_osc(i - 5)
-            if hd + 1 < B * H:
-                if r == 3:
+                if (i - 4) % R == R - 1:
+                    st_rcp((i - 4) // R)
+            if ok(i - 8):
+                st_osc(i - 8)
+            if hd + 1 < NH:
+                if t == 3:
                     prep_q(hd + 1)
                     prep_v(hd + 1)
-                if r == 4:
+                if t == 4:
                     prep_k(hd + 1)
                     quant_v(hd + 1)
-            if ok(i - 6) and (i - 6) % NQ == NQ - 1:
-                nc.sync.dma_start(out=o_v[(i - 6) // NQ], in_=hdt[("o", (i - 6) // NQ)][:])
+            if ok(i - 9) and (i - 9) % R == R - 1:
+                nc.sync.dma_start(out=o_v[(i - 9) // R], in_=tl[("ob", (i - 9) // R)][:])

@@ -117,8 +117,7 @@ def tile_gpsdpattention_t_kernel(tc, Q, K, V, attn_mask, out):
         def prep_v(hd):
             vg = hd_pool.tile([P, 2, D, 4], BF16, name="vg", align_bytes=64)
             for c in range(2):
-                nc.gpsimd.tensor_scalar(out=vg[:, c], in0=raw[hd][2][:, c].rearrange("p t d -> p d t"),
-                                        scalar1=1.0, scalar2=0.0, op0=ALU.mult, op1=ALU.add)
+                nc.scalar.copy(out=vg[:, c], in_=raw[hd][2][:, c].rearrange("p t d -> p d t"))
             hdt[("vg", hd)] = vg
 
         def quant_v(hd):
@@ -242,6 +241,10 @@ def tile_gpsdpattention_t_kernel(tc, Q, K, V, attn_mask, out):
             if ok(i):
                 st_mask(i)
                 st_band(i)
+            if ok(i - 4):
+                st_qnt(i - 4)
+                if (i - 4) % R == R - 1:
+                    st_rcp((i - 4) // R)
             if ok(i - 1):
                 st_max(i - 1)
             if ok(i - 2):
@@ -249,10 +252,6 @@ def tile_gpsdpattention_t_kernel(tc, Q, K, V, attn_mask, out):
                 st_tr(i - 2)
             if ok(i - 3):
                 st_cpy(i - 3)
-            if ok(i - 4):
-                st_qnt(i - 4)
-                if (i - 4) % R == R - 1:
-                    st_rcp((i - 4) // R)
             if ok(i - 8):
                 st_osc(i - 8)
             if hd + 1 < NH:

@@ -16,16 +16,17 @@ AX = mybir.AxisListType
 
 B, H, S, D = 4, 4, 1024, 128
 P = 128
-R = 4
+R = 2
 GQ = P * R
 NG = B * H * S // GQ
 NT = NG * R
 NH = B * H
+TPH = S // P
 SIGMAS = (5.0, 10.0, 20.0, 40.0)
 FLOPS = 2 * 2 * B * H * S * S * D
 SCALE = 1.0 / math.sqrt(D)
 BIG = 2.0 ** 100
-MASK_BUFS = 3
+MASK_BUFS = 5
 
 
 def reach(sigma):
@@ -47,8 +48,9 @@ def tile_gpsdpattention_t_kernel(tc, Q, K, V, attn_mask, out):
         ld = ctx.enter_context(tc.tile_pool(name="ld", bufs=2))
         mk = ctx.enter_context(tc.tile_pool(name="mk", bufs=MASK_BUFS))
         hd_pool = ctx.enter_context(tc.tile_pool(name="hd", bufs=2))
-        gp = ctx.enter_context(tc.tile_pool(name="gp", bufs=3))
+        gp = ctx.enter_context(tc.tile_pool(name="gp", bufs=4))
         wk = ctx.enter_context(tc.tile_pool(name="wk", bufs=4))
+        ek = ctx.enter_context(tc.tile_pool(name="ek", bufs=4))
         small = ctx.enter_context(tc.tile_pool(name="small", bufs=8))
         ps_s = ctx.enter_context(tc.psum_pool(name="ps_s", bufs=4))
         ps_t = ctx.enter_context(tc.psum_pool(name="ps_t", bufs=2))
@@ -99,18 +101,18 @@ def tile_gpsdpattention_t_kernel(tc, Q, K, V, attn_mask, out):
             prior.append((lp, tab))
 
         def prep_q(hd):
-            qT_ps = ps_t.tile([P, S // P, P], BF16, name="qT_ps", tag="tr")
-            for t in range(S // P):
+            qT_ps = ps_t.tile([P, TPH, P], BF16, name="qT_ps", tag="tr")
+            for t in range(TPH):
                 nc.tensor.transpose(qT_ps[:, t, :], raw[hd][0][:, t // R, t % R, :], ident[:])
-            qT = hd_pool.tile([P, S // P, P], BF16, name="qT")
+            qT = hd_pool.tile([P, TPH, P], BF16, name="qT")
             nc.scalar.copy(out=qT[:], in_=qT_ps[:])
             hdt[("q", hd)] = qT
 
         def prep_k(hd):
-            kT_ps = ps_t.tile([P, S // P, P], BF16, name="kT_ps", tag="tr")
-            for a in range(S // P):
+            kT_ps = ps_t.tile([P, TPH, P], BF16, name="kT_ps", tag="tr")
+            for a in range(TPH):
                 nc.tensor.transpose(kT_ps[:, a, :], raw[hd][1][:, a, :], ident[:])
-            kT = hd_pool.tile([P, P, S // P], BF16, name="kT")
+            kT = hd_pool.tile([P, P, TPH], BF16, name="kT")
             nc.scalar.copy(out=kT[:], in_=kT_ps[:].rearrange("d a p -> d p a"))
             hdt[("k", hd)] = kT
 
@@ -128,7 +130,7 @@ def tile_gpsdpattention_t_kernel(tc, Q, K, V, attn_mask, out):
             hdt[("v", hd)] = (vc, vs)
 
         def st_qk(n):
-            hd, t = divmod(n, S // P)
+            hd, t = divmod(n, TPH)
             kT = hdt[("k", hd)][:].rearrange("d p a -> d (p a)")
             banks = []
             for c in range(2):
@@ -139,38 +141,41 @@ def tile_gpsdpattention_t_kernel(tc, Q, K, V, attn_mask, out):
             tl[("sc", n)] = banks
 
         def st_mask(n):
-            m_k = tl[("m", n // R)][:, n % R, :].rearrange("p (k w) -> p k w", w=2)
-            sm = wk.tile([P, S], F32, name="sm")
+            g, r = divmod(n, R)
+            m_k = tl[("m", g)][:, r, :].rearrange("p (k w) -> p k w", w=2)
+            if r == 0:
+                tl[("sm", g)] = wk.tile([P, R, S], F32, name="sm")
             for c in range(2):
                 cols = slice(c * (S // 2), (c + 1) * (S // 2))
-                nc.vector.scalar_tensor_tensor(out=sm[:, cols], in0=m_k[:, cols, 0], scalar=-BIG,
+                nc.vector.scalar_tensor_tensor(out=tl[("sm", g)][:, r, cols], in0=m_k[:, cols, 0], scalar=-BIG,
                                                in1=tl[("sc", n)][c][:], op0=ALU.mult, op1=ALU.add)
-            tl[("sm", n)] = sm
 
         def st_band(n):
             g, r = divmod(n, R)
             lp, tab = prior[(g // (S // GQ)) % H]
-            sm = tl[("sm", n)]
+            sm = tl[("sm", g)]
             j_hi = GQ * (g % (S // GQ)) + GQ
             j_lo = max(0, j_hi - GQ - lp)
             z_hi = GQ + lp + R - 1 - r
-            nc.gpsimd.tensor_tensor(out=sm[:, j_lo:j_hi], in0=sm[:, j_lo:j_hi],
+            nc.gpsimd.tensor_tensor(out=sm[:, r, j_lo:j_hi], in0=sm[:, r, j_lo:j_hi],
                                     in1=tab[:, z_hi - (j_hi - j_lo):z_hi], op=ALU.add)
 
-        def st_max(n):
-            negm = small.tile([P, 1], F32, name="negm")
-            nc.vector.tensor_reduce(out=negm[:], in_=tl[("sm", n)][:], axis=AX.X, op=ALU.max, negate=True)
-            tl[("negm", n)] = negm
+        def st_max(g):
+            negm = small.tile([P, R], F32, name="negm")
+            nc.vector.tensor_reduce(out=negm[:], in_=tl[("sm", g)][:], axis=AX.X, op=ALU.max, negate=True)
+            tl[("negm", g)] = negm
+
+        def st_bias(g):
+            bias = small.tile([P, R], F32, name="bias")
+            nc.scalar.mul(out=bias[:], in_=tl[("negm", g)][:], mul=SCALE)
+            tl[("bias", g)] = bias
+            tl[("rs", g)] = gp.tile([P, R], F32, name="rs")
 
         def st_exp(n):
             g, r = divmod(n, R)
-            bias = small.tile([P, 1], F32, name="bias")
-            nc.scalar.mul(out=bias[:], in_=tl[("negm", n)][:], mul=SCALE)
-            if r == 0:
-                tl[("rs", g)] = gp.tile([P, R], F32, name="rs")
-            e = wk.tile([P, S], BF16, name="e")
-            nc.scalar.activation(out=e[:], in_=tl[("sm", n)][:], func=ACT.Exp, bias=bias[:], scale=SCALE,
-                                 accum_out=tl[("rs", g)][:, r:r + 1])
+            e = ek.tile([P, S], BF16, name="e")
+            nc.scalar.activation(out=e[:], in_=tl[("sm", g)][:, r, :], func=ACT.Exp, bias=tl[("bias", g)][:, r:r + 1],
+                                 scale=SCALE, accum_out=tl[("rs", g)][:, r:r + 1])
             tl[("e", n)] = e
 
         def st_tr(n):
@@ -182,84 +187,96 @@ def tile_gpsdpattention_t_kernel(tc, Q, K, V, attn_mask, out):
             tl[("eT", n)] = eT
 
         def st_cpy(n):
-            eg = wk.tile([P, 2, P, 4], BF16, name="eg", align_bytes=64)
-            nc.scalar.copy(out=eg[:].bitcast(F32), in_=tl[("eT", n)][:].rearrange("p c u q -> p c q u"))
-            tl[("eg", n)] = eg
+            g, r = divmod(n, R)
+            if r == 0:
+                tl[("eg", g)] = wk.tile([P, R, 2, P, 4], BF16, name="eg", align_bytes=64)
+            nc.scalar.copy(out=tl[("eg", g)][:, r].bitcast(F32), in_=tl[("eT", n)][:].rearrange("p c u q -> p c q u"))
 
-        def st_qnt(n):
-            ec = wk.tile([P, 2 * P], U32, name="ec", align_bytes=64)
-            es = wk.tile([P, 2 * P], U8, name="es", align_bytes=64)
+        def st_qnt(g):
+            ec = wk.tile([P, R * 2 * P], U32, name="ec", align_bytes=64)
+            es = wk.tile([P, R * 2 * P], U8, name="es", align_bytes=64)
             nc.vector.quantize_mx(out=ec[:].bitcast(FP8X4), scales=es[:],
-                                  in_=tl[("eg", n)][:].rearrange("p c q t -> p (c q t)"))
-            tl[("ec", n)] = (ec, es)
-
-        def st_rcp(g):
+                                  in_=tl[("eg", g)][:].rearrange("p r c q t -> p (r c q t)"))
+            tl[("ec", g)] = (ec, es)
             rinv = gp.tile([P, R], F32, name="rinv")
             nc.vector.reciprocal(rinv[:], tl[("rs", g)][:])
             tl[("rinv", g)] = rinv
 
-        def st_mx(n):
-            g, r = divmod(n, R)
-            vc, vs = hdt[("v", n // (S // P))]
-            ec, es = tl[("ec", n)]
-            if r == 0:
-                tl[("o", g)] = ps_o.tile([P, R, D], F32, name="o_ps")
-            for c in range(2):
-                cols = slice(c * P, (c + 1) * P)
-                nc.tensor.matmul_mx(out=tl[("o", g)][:, r, :], lhsT=ec[:, cols].bitcast(FP8X4), lhsT_scale=es[:, cols],
-                                    rhs=vc[:, cols].bitcast(FP8X4), rhs_scale=vs[:, cols],
-                                    start=(c == 0), stop=(c == 1))
+        def st_mx(g):
+            vc, vs = hdt[("v", g // (S // GQ))]
+            ec, es = tl[("ec", g)]
+            o_ps = ps_o.tile([P, R, D], F32, name="o_ps")
+            for r in range(R):
+                for c in range(2):
+                    ecols = slice((2 * r + c) * P, (2 * r + c + 1) * P)
+                    vcols = slice(c * P, (c + 1) * P)
+                    nc.tensor.matmul_mx(out=o_ps[:, r, :], lhsT=ec[:, ecols].bitcast(FP8X4), lhsT_scale=es[:, ecols],
+                                        rhs=vc[:, vcols].bitcast(FP8X4), rhs_scale=vs[:, vcols],
+                                        start=(c == 0), stop=(c == 1))
+            tl[("o", g)] = o_ps
 
-        def st_osc(n):
-            g, r = divmod(n, R)
-            if r == 0:
-                tl[("ob", g)] = gp.tile([P, R, D], F32, name="o_sb")
-            nc.scalar.activation(out=tl[("ob", g)][:, r, :], in_=tl[("o", g)][:, r, :], func=ACT.Copy,
-                                 scale=tl[("rinv", g)][:, r:r + 1])
+        def st_osc(g):
+            o_sb = gp.tile([P, R, D], F32, name="o_sb")
+            for r in range(R):
+                nc.scalar.activation(out=o_sb[:, r, :], in_=tl[("o", g)][:, r, :], func=ACT.Copy,
+                                     scale=tl[("rinv", g)][:, r:r + 1])
+            tl[("ob", g)] = o_sb
 
-        def ok(n):
-            return 0 <= n < NT
+        def okg(g):
+            return 0 <= g < NG
 
-        load_mask(1, 1)
+        for g in range(1, MASK_BUFS - 1):
+            load_mask(g, 1)
         load_head(1)
         prep_q(0)
         prep_k(0)
         prep_v(0)
         quant_v(0)
         st_qk(0)
-        TPH = S // P
-        for i in range(NT + 13):
-            hd, t = divmod(i, TPH)
-            if i % R == 0 and i // R + 2 < NG:
-                load_mask(i // R + 2, 1)
-            if t == 1 and hd + 2 < NH:
+        st_qk(1)
+        GPH = S // GQ
+        for j in range(NG + 6):
+            hd, gl = divmod(j, GPH)
+            if okg(j + MASK_BUFS - 1):
+                load_mask(j + MASK_BUFS - 1, 1)
+            if gl == 0 and hd + 2 < NH:
                 load_head(hd + 2)
-            if ok(i - 5):
-                st_mx(i - 5)
-            if ok(i + 1):
-                st_qk(i + 1)
-            if ok(i):
-                st_mask(i)
-                st_band(i)
-            if ok(i - 4):
-                st_qnt(i - 4)
-                if (i - 4) % R == R - 1:
-                    st_rcp((i - 4) // R)
-            if ok(i - 1):
-                st_max(i - 1)
-            if ok(i - 2):
-                st_exp(i - 2)
-                st_tr(i - 2)
-            if ok(i - 3):
-                st_cpy(i - 3)
-            if ok(i - 8):
-                st_osc(i - 8)
+            if okg(j - 4):
+                st_mx(j - 4)
+            if okg(j):
+                st_mask(2 * j)
+                st_band(2 * j)
+            if okg(j + 1):
+                st_qk(2 * j + 2)
+            if okg(j):
+                st_mask(2 * j + 1)
+                st_band(2 * j + 1)
+            if okg(j - 2):
+                st_bias(j - 2)
+                st_exp(2 * j - 4)
+                st_tr(2 * j - 4)
+            if okg(j + 1):
+                st_qk(2 * j + 3)
+            if okg(j - 2):
+                st_exp(2 * j - 3)
+                st_tr(2 * j - 3)
+            if okg(j - 1):
+                st_max(j - 1)
+            if okg(j - 2):
+                st_cpy(2 * j - 4)
+            if okg(j - 4):
+                st_osc(j - 4)
+            if okg(j - 2):
+                st_cpy(2 * j - 3)
+            if okg(j - 3):
+                st_qnt(j - 3)
             if hd + 1 < NH:
-                if t == 3:
+                if gl == 1:
                     prep_q(hd + 1)
-                    prep_v(hd + 1)
-                if t == 4:
+                if gl == 2:
                     prep_k(hd + 1)
+                    prep_v(hd + 1)
+                if gl == 3:
                     quant_v(hd + 1)
-            if ok(i - 9) and (i - 9) % R == R - 1:
-                nc.sync.dma_start(out=o_v[(i - 9) // R], in_=tl[("ob", (i - 9) // R)][:])
+            if okg(j - 5):
+                nc.sync.dma_start(out=o_v[j - 5], in_=tl[("ob", j - 5)][:])

@@ -101,19 +101,25 @@ def tile_gpsdpattention_t_kernel(tc, Q, K, V, attn_mask, out):
             prior.append((lp, tab))
 
         def prep_q(hd):
-            qT_ps = ps_t.tile([P, TPH, P], BF16, name="qT_ps", tag="tr")
+            qT_ps = ps_o.tile([P, TPH, P], BF16, name="qT_ps", tag="o_ps")
             for t in range(TPH):
                 nc.tensor.transpose(qT_ps[:, t, :], raw[hd][0][:, t // R, t % R, :], ident[:])
+            hdt[("qp", hd)] = qT_ps
+
+        def copy_q(hd):
             qT = hd_pool.tile([P, TPH, P], BF16, name="qT")
-            nc.scalar.copy(out=qT[:], in_=qT_ps[:])
+            nc.scalar.copy(out=qT[:], in_=hdt[("qp", hd)][:])
             hdt[("q", hd)] = qT
 
         def prep_k(hd):
-            kT_ps = ps_t.tile([P, TPH, P], BF16, name="kT_ps", tag="tr")
+            kT_ps = ps_o.tile([P, TPH, P], BF16, name="kT_ps", tag="o_ps")
             for a in range(TPH):
                 nc.tensor.transpose(kT_ps[:, a, :], raw[hd][1][:, a, :], ident[:])
+            hdt[("kp", hd)] = kT_ps
+
+        def copy_k(hd):
             kT = hd_pool.tile([P, P, TPH], BF16, name="kT")
-            nc.scalar.copy(out=kT[:], in_=kT_ps[:].rearrange("d a p -> d p a"))
+            nc.scalar.copy(out=kT[:], in_=hdt[("kp", hd)][:].rearrange("d a p -> d p a"))
             hdt[("k", hd)] = kT
 
         def prep_v(hd):
@@ -229,20 +235,27 @@ def tile_gpsdpattention_t_kernel(tc, Q, K, V, attn_mask, out):
             load_mask(g, 1)
         load_head(1)
         prep_q(0)
+        copy_q(0)
         prep_k(0)
+        copy_k(0)
         prep_v(0)
         quant_v(0)
         st_qk(0)
         st_qk(1)
         GPH = S // GQ
-        for j in range(NG + 6):
+        for j in range(NG + 7):
             hd, gl = divmod(j, GPH)
+            nxt = hd + 1 < NH
             if okg(j + MASK_BUFS - 1):
                 load_mask(j + MASK_BUFS - 1, 1)
             if gl == 0 and hd + 2 < NH:
                 load_head(hd + 2)
-            if okg(j - 4):
-                st_mx(j - 4)
+            if okg(j - 5):
+                st_mx(j - 5)
+            if nxt and gl == 1:
+                prep_q(hd + 1)
+            if nxt and gl == 2:
+                prep_k(hd + 1)
             if okg(j):
                 st_mask(2 * j)
                 st_band(2 * j)
@@ -251,32 +264,31 @@ def tile_gpsdpattention_t_kernel(tc, Q, K, V, attn_mask, out):
             if okg(j):
                 st_mask(2 * j + 1)
                 st_band(2 * j + 1)
-            if okg(j - 2):
-                st_bias(j - 2)
-                st_exp(2 * j - 4)
-                st_tr(2 * j - 4)
             if okg(j + 1):
                 st_qk(2 * j + 3)
             if okg(j - 2):
+                st_bias(j - 2)
+                st_exp(2 * j - 4)
                 st_exp(2 * j - 3)
-                st_tr(2 * j - 3)
             if okg(j - 1):
                 st_max(j - 1)
-            if okg(j - 2):
-                st_cpy(2 * j - 4)
-            if okg(j - 4):
-                st_osc(j - 4)
-            if okg(j - 2):
-                st_cpy(2 * j - 3)
             if okg(j - 3):
-                st_qnt(j - 3)
-            if hd + 1 < NH:
+                st_cpy(2 * j - 6)
+                st_cpy(2 * j - 5)
+            if okg(j - 2):
+                st_tr(2 * j - 4)
+                st_tr(2 * j - 3)
+            if okg(j - 5):
+                st_osc(j - 5)
+            if okg(j - 4):
+                st_qnt(j - 4)
+            if nxt:
                 if gl == 1:
-                    prep_q(hd + 1)
+                    copy_q(hd + 1)
                 if gl == 2:
-                    prep_k(hd + 1)
+                    copy_k(hd + 1)
                     prep_v(hd + 1)
                 if gl == 3:
                     quant_v(hd + 1)
-            if okg(j - 5):
-                nc.sync.dma_start(out=o_v[j - 5], in_=tl[("ob", j - 5)][:])
+            if okg(j - 6):
+                nc.sync.dma_start(out=o_v[j - 6], in_=tl[("ob", j - 6)][:])

@@ -48,6 +48,7 @@ def tile_gpsdpattention_t_kernel(tc, Q, K, V, attn_mask, out):
         ld = ctx.enter_context(tc.tile_pool(name="ld", bufs=2))
         mk = ctx.enter_context(tc.tile_pool(name="mk", bufs=MASK_BUFS))
         hd_pool = ctx.enter_context(tc.tile_pool(name="hd", bufs=2))
+        vq = ctx.enter_context(tc.tile_pool(name="vq", bufs=3))
         gp = ctx.enter_context(tc.tile_pool(name="gp", bufs=4))
         wk = ctx.enter_context(tc.tile_pool(name="wk", bufs=4))
         ek = ctx.enter_context(tc.tile_pool(name="ek", bufs=4))
@@ -129,8 +130,8 @@ def tile_gpsdpattention_t_kernel(tc, Q, K, V, attn_mask, out):
             hdt[("vg", hd)] = vg
 
         def quant_v(hd):
-            vc = hd_pool.tile([P, 2 * D], U32, name="vc", align_bytes=64)
-            vs = hd_pool.tile([P, 2 * D], U8, name="vs", align_bytes=64)
+            vc = vq.tile([P, 2 * D], U32, name="vc", align_bytes=64)
+            vs = vq.tile([P, 2 * D], U8, name="vs", align_bytes=64)
             nc.vector.quantize_mx(out=vc[:].bitcast(FP8X4), scales=vs[:],
                                   in_=hdt[("vg", hd)][:].rearrange("p c d t -> p (c d t)"))
             hdt[("v", hd)] = (vc, vs)

@@ -27,6 +27,7 @@ FLOPS = 2 * 2 * B * H * S * S * D
 SCALE = 1.0 / math.sqrt(D)
 BIG = 2.0 ** 100
 MASK_BUFS = 5
+OUT_BUFS = 40
 
 
 def reach(sigma):
@@ -50,6 +51,7 @@ def tile_gpsdpattention_t_kernel(tc, Q, K, V, attn_mask, out):
         hd_pool = ctx.enter_context(tc.tile_pool(name="hd", bufs=2))
         vq = ctx.enter_context(tc.tile_pool(name="vq", bufs=3))
         gp = ctx.enter_context(tc.tile_pool(name="gp", bufs=4))
+        ob = ctx.enter_context(tc.tile_pool(name="ob", bufs=OUT_BUFS))
         wk = ctx.enter_context(tc.tile_pool(name="wk", bufs=4))
         ek = ctx.enter_context(tc.tile_pool(name="ek", bufs=4))
         small = ctx.enter_context(tc.tile_pool(name="small", bufs=8))
@@ -223,7 +225,7 @@ def tile_gpsdpattention_t_kernel(tc, Q, K, V, attn_mask, out):
             tl[("o", g)] = o_ps
 
         def st_osc(g):
-            o_sb = gp.tile([P, R, D], F32, name="o_sb")
+            o_sb = ob.tile([P, R, D], F32, name="o_sb")
             for r in range(R):
                 nc.scalar.activation(out=o_sb[:, r, :], in_=tl[("o", g)][:, r, :], func=ACT.Copy,
                                      scale=tl[("rinv", g)][:, r:r + 1])
@@ -244,11 +246,21 @@ def tile_gpsdpattention_t_kernel(tc, Q, K, V, attn_mask, out):
         st_qk(0)
         st_qk(1)
         GPH = S // GQ
+
+        def store(g):
+            nc.sync.dma_start(out=o_v[g], in_=tl[("ob", g)][:])
+
+        last_load = NG - MASK_BUFS
+        first_held = last_load - 5 - OUT_BUFS + 3
+        held = []
         for j in range(NG + 7):
             hd, gl = divmod(j, GPH)
             nxt = hd + 1 < NH
             if okg(j + MASK_BUFS - 1):
                 load_mask(j + MASK_BUFS - 1, 1)
+            if j == last_load:
+                for g in held:
+                    store(g)
             if gl == 0 and hd + 2 < NH:
                 load_head(hd + 2)
             if okg(j - 5):
@@ -292,4 +304,7 @@ def tile_gpsdpattention_t_kernel(tc, Q, K, V, attn_mask, out):
                 if gl == 3:
                     quant_v(hd + 1)
             if okg(j - 6):
-                nc.sync.dma_start(out=o_v[j - 6], in_=tl[("ob", j - 6)][:])
+                if first_held <= j - 6 and j < last_load:
+                    held.append(j - 6)
+                else:
+                    store(j - 6)

@@ -27,7 +27,8 @@ FLOPS = 2 * 2 * B * H * S * S * D
 SCALE = 1.0 / math.sqrt(D)
 BIG = 2.0 ** 100
 MASK_BUFS = 5
-OUT_BUFS = 40
+OUT_BUFS = 41
+LAST_IN_S = 2
 
 
 def reach(sigma):
@@ -53,6 +54,7 @@ def tile_gpsdpattention_t_kernel(tc, Q, K, V, attn_mask, out):
         gp = ctx.enter_context(tc.tile_pool(name="gp", bufs=4))
         ob = ctx.enter_context(tc.tile_pool(name="ob", bufs=OUT_BUFS))
         wk = ctx.enter_context(tc.tile_pool(name="wk", bufs=4))
+        wq = ctx.enter_context(tc.tile_pool(name="wq", bufs=3))
         ek = ctx.enter_context(tc.tile_pool(name="ek", bufs=4))
         small = ctx.enter_context(tc.tile_pool(name="small", bufs=8))
         ps_s = ctx.enter_context(tc.psum_pool(name="ps_s", bufs=4))
@@ -63,14 +65,25 @@ def tile_gpsdpattention_t_kernel(tc, Q, K, V, attn_mask, out):
         hdt = {}
         tl = {}
 
-        def load_head(hd):
+        def load_q(hd):
             q_raw = ld.tile([P, S // GQ, R, D], BF16, name="q_raw")
             nc.sync.dma_start(out=q_raw[:], in_=q_v[hd])
+            raw[("q", hd)] = q_raw
+
+        def load_k(hd):
             k_raw = ld.tile([P, S // P, D], BF16, name="k_raw")
             nc.sync.dma_start(out=k_raw[:], in_=k_v[hd])
+            raw[("k", hd)] = k_raw
+
+        def load_v(hd):
             v_raw = ld.tile([P, 2, 4, D], BF16, name="v_raw")
             nc.sync.dma_start(out=v_raw[:], in_=v_v[hd])
-            raw[hd] = (q_raw, k_raw, v_raw)
+            raw[("v", hd)] = v_raw
+
+        def load_head(hd):
+            load_q(hd)
+            load_k(hd)
+            load_v(hd)
 
         def load_mask(g, pieces):
             m_raw = mk.tile([P, R, 2 * S], I32, name="m_raw")
@@ -79,34 +92,54 @@ def tile_gpsdpattention_t_kernel(tc, Q, K, V, attn_mask, out):
                 nc.sync.dma_start(out=m_raw[:, j * step:(j + 1) * step, :], in_=m_v[g, :, j * step:(j + 1) * step, :])
             tl[("m", g)] = m_raw
 
-        load_head(0)
+        load_k(0)
+        load_q(0)
         load_mask(0, R)
+        load_mask(1, 1)
+        load_q(1)
+        load_mask(2, 1)
+        load_k(1)
+        load_v(0)
+        load_mask(3, 1)
+        load_v(1)
+
+        warm = const.tile([P, 1], F32, name="warm")
+        nc.vector.memset(warm[:], 0.0)
+        nc.scalar.activation(out=warm[:], in_=warm[:], func=ACT.Exp)
 
         ident = const.tile([P, P], BF16, name="ident")
         make_identity(nc, ident[:])
-        ident_f = const.tile([P, P], F32, name="ident_f")
-        make_identity(nc, ident_f[:])
 
-        prior = []
-        for h in range(H):
+        prior = {}
+        pscr = {}
+
+        def prior_dist(h):
             lp = reach(SIGMAS[h])
             wt = GQ + R - 1 + lp
-            d_i = const.tile([P, wt], I32, name="d_i", tag="d_i")
-            nc.gpsimd.iota(d_i[:], pattern=[[-1, wt]], base=lp + R - 1, channel_multiplier=R)
             d_f = const.tile([P, wt], F32, name="d_f", tag="d_f")
-            nc.vector.tensor_copy(out=d_f[:], in_=d_i[:])
+            nc.gpsimd.iota(d_f[:], pattern=[[-1, wt]], base=lp + R - 1, channel_multiplier=R,
+                           allow_small_or_imprecise_dtypes=True)
             g_t = const.tile([P, wt], F32, name="g_t", tag="g_t")
             nc.scalar.activation(out=g_t[:], in_=d_f[:], func=ACT.Square)
             nc.scalar.activation(out=g_t[:], in_=g_t[:], func=ACT.Exp, scale=-1.0 / (2.0 * SIGMAS[h] ** 2))
-            nc.vector.scalar_tensor_tensor(out=g_t[:], in0=d_f[:], scalar=0.0, in1=g_t[:], op0=ALU.is_ge, op1=ALU.mult)
-            tab = const.tile([P, wt], F32, name="tab%d" % h)
-            nc.vector.tensor_scalar_mul(out=tab[:], in0=g_t[:], scalar1=math.sqrt(D))
-            prior.append((lp, tab))
+            pscr[h] = (d_f, g_t)
+
+        def prior_table(h):
+            d_f, g_t = pscr[h]
+            nc.gpsimd.tensor_scalar(out=d_f[:], in0=d_f[:], scalar1=0.0, scalar2=math.sqrt(D), op0=ALU.is_ge, op1=ALU.mult)
+            tab = const.tile([P, d_f.shape[1]], F32, name="tab%d" % h)
+            nc.gpsimd.tensor_tensor(out=tab[:], in0=d_f[:], in1=g_t[:], op=ALU.mult)
+            prior[h] = (reach(SIGMAS[h]), tab)
+
+        prior_dist(0)
+        prior_table(0)
+        ident_f = const.tile([P, P], F32, name="ident_f")
+        make_identity(nc, ident_f[:])
 
         def prep_q(hd):
             qT_ps = ps_o.tile([P, TPH, P], BF16, name="qT_ps", tag="o_ps")
             for t in range(TPH):
-                nc.tensor.transpose(qT_ps[:, t, :], raw[hd][0][:, t // R, t % R, :], ident[:])
+                nc.tensor.transpose(qT_ps[:, t, :], raw[("q", hd)][:, t // R, t % R, :], ident[:])
             hdt[("qp", hd)] = qT_ps
 
         def copy_q(hd):
@@ -117,7 +150,7 @@ def tile_gpsdpattention_t_kernel(tc, Q, K, V, attn_mask, out):
         def prep_k(hd):
             kT_ps = ps_o.tile([P, TPH, P], BF16, name="kT_ps", tag="o_ps")
             for a in range(TPH):
-                nc.tensor.transpose(kT_ps[:, a, :], raw[hd][1][:, a, :], ident[:])
+                nc.tensor.transpose(kT_ps[:, a, :], raw[("k", hd)][:, a, :], ident[:])
             hdt[("kp", hd)] = kT_ps
 
         def copy_k(hd):
@@ -128,7 +161,7 @@ def tile_gpsdpattention_t_kernel(tc, Q, K, V, attn_mask, out):
         def prep_v(hd):
             vg = hd_pool.tile([P, 2, D, 4], BF16, name="vg", align_bytes=64)
             for c in range(2):
-                nc.scalar.copy(out=vg[:, c], in_=raw[hd][2][:, c].rearrange("p t d -> p d t"))
+                nc.scalar.copy(out=vg[:, c], in_=raw[("v", hd)][:, c].rearrange("p t d -> p d t"))
             hdt[("vg", hd)] = vg
 
         def quant_v(hd):
@@ -178,7 +211,9 @@ def tile_gpsdpattention_t_kernel(tc, Q, K, V, attn_mask, out):
             bias = small.tile([P, R], F32, name="bias")
             nc.scalar.mul(out=bias[:], in_=tl[("negm", g)][:], mul=SCALE)
             tl[("bias", g)] = bias
-            tl[("rs", g)] = gp.tile([P, R], F32, name="rs")
+            if g % 2 == 0:
+                tl[("rs2", g // 2)] = gp.tile([P, 2, R], F32, name="rs")
+            tl[("rs", g)] = tl[("rs2", g // 2)][:, g % 2, :]
 
         def st_exp(n):
             g, r = divmod(n, R)
@@ -188,7 +223,10 @@ def tile_gpsdpattention_t_kernel(tc, Q, K, V, attn_mask, out):
             tl[("e", n)] = e
 
         def st_tr(n):
-            eT = ps_t.tile([P, 2, 2, P], F32, name="eT", tag="tr")
+            if n >= R * (NG - LAST_IN_S):
+                eT = ps_s.tile([P, 2, 2, P], F32, name="eT", tag="sc")
+            else:
+                eT = ps_t.tile([P, 2, 2, P], F32, name="eT", tag="tr")
             e_w = tl[("e", n)][:].bitcast(F32).rearrange("q (c k u) -> q c u k", c=2, u=2)
             for c in range(2):
                 for u in range(2):
@@ -198,18 +236,20 @@ def tile_gpsdpattention_t_kernel(tc, Q, K, V, attn_mask, out):
         def st_cpy(n):
             g, r = divmod(n, R)
             if r == 0:
-                tl[("eg", g)] = wk.tile([P, R, 2, P, 4], BF16, name="eg", align_bytes=64)
+                tl[("eg", g)] = wq.tile([P, R, 2, P, 4], BF16, name="eg", align_bytes=64)
             nc.scalar.copy(out=tl[("eg", g)][:, r].bitcast(F32), in_=tl[("eT", n)][:].rearrange("p c u q -> p c q u"))
 
         def st_qnt(g):
-            ec = wk.tile([P, R * 2 * P], U32, name="ec", align_bytes=64)
-            es = wk.tile([P, R * 2 * P], U8, name="es", align_bytes=64)
+            if g % 2 == 0:
+                rinv = gp.tile([P, 2, R], F32, name="rinv")
+                nc.vector.reciprocal(rinv[:], tl[("rs2", g // 2)][:])
+                tl[("rinv", g)] = rinv[:, 0, :]
+                tl[("rinv", g + 1)] = rinv[:, 1, :]
+            ec = wq.tile([P, R * 2 * P], U32, name="ec", align_bytes=64)
+            es = wq.tile([P, R * 2 * P], U8, name="es", align_bytes=64)
             nc.vector.quantize_mx(out=ec[:].bitcast(FP8X4), scales=es[:],
                                   in_=tl[("eg", g)][:].rearrange("p r c q t -> p (r c q t)"))
             tl[("ec", g)] = (ec, es)
-            rinv = gp.tile([P, R], F32, name="rinv")
-            nc.vector.reciprocal(rinv[:], tl[("rs", g)][:])
-            tl[("rinv", g)] = rinv
 
         def st_mx(g):
             vc, vs = hdt[("v", g // (S // GQ))]
@@ -234,15 +274,10 @@ def tile_gpsdpattention_t_kernel(tc, Q, K, V, attn_mask, out):
         def okg(g):
             return 0 <= g < NG
 
-        for g in range(1, MASK_BUFS - 1):
-            load_mask(g, 1)
-        load_head(1)
-        prep_q(0)
-        copy_q(0)
         prep_k(0)
         copy_k(0)
-        prep_v(0)
-        quant_v(0)
+        prep_q(0)
+        copy_q(0)
         st_qk(0)
         st_qk(1)
         GPH = S // GQ
@@ -251,9 +286,11 @@ def tile_gpsdpattention_t_kernel(tc, Q, K, V, attn_mask, out):
             nc.sync.dma_start(out=o_v[g], in_=tl[("ob", g)][:])
 
         last_load = NG - MASK_BUFS
-        first_held = last_load - 5 - OUT_BUFS + 3
+        first_held = last_load - 6 - OUT_BUFS + 3
         held = []
-        for j in range(NG + 7):
+        junk_f = const.tile([P, 1], F32, name="junk_f")
+        junk_u = const.tile([P, 1], U32, name="junk_u")
+        for j in range(NG + 8):
             hd, gl = divmod(j, GPH)
             nxt = hd + 1 < NH
             if okg(j + MASK_BUFS - 1):
@@ -263,48 +300,61 @@ def tile_gpsdpattention_t_kernel(tc, Q, K, V, attn_mask, out):
                     store(g)
             if gl == 0 and hd + 2 < NH:
                 load_head(hd + 2)
-            if okg(j - 5):
-                st_mx(j - 5)
+            if okg(j - 6):
+                st_mx(j - 6)
             if nxt and gl == 1:
                 prep_q(hd + 1)
             if nxt and gl == 2:
                 prep_k(hd + 1)
+            if okg(j - 6):
+                nc.gpsimd.tensor_copy(out=junk_u[:], in_=tl[("ec", j - 6)][0][:, 0:1])
+            elif okg(j - 3):
+                nc.gpsimd.tensor_copy(out=junk_f[:], in_=tl[("negm", j - 3)][:, 0:1])
+            if okg(j - 1):
+                st_band(2 * j - 2)
+                st_band(2 * j - 1)
             if okg(j):
                 st_mask(2 * j)
-                st_band(2 * j)
             if okg(j + 1):
                 st_qk(2 * j + 2)
             if okg(j):
                 st_mask(2 * j + 1)
-                st_band(2 * j + 1)
             if okg(j + 1):
                 st_qk(2 * j + 3)
-            if okg(j - 2):
-                st_bias(j - 2)
-                st_exp(2 * j - 4)
-                st_exp(2 * j - 3)
-            if okg(j - 1):
-                st_max(j - 1)
             if okg(j - 3):
-                st_cpy(2 * j - 6)
-                st_cpy(2 * j - 5)
+                st_bias(j - 3)
+                st_exp(2 * j - 6)
+                st_exp(2 * j - 5)
             if okg(j - 2):
-                st_tr(2 * j - 4)
-                st_tr(2 * j - 3)
-            if okg(j - 5):
-                st_osc(j - 5)
+                st_max(j - 2)
             if okg(j - 4):
-                st_qnt(j - 4)
+                st_cpy(2 * j - 8)
+                st_cpy(2 * j - 7)
+            if okg(j - 3):
+                st_tr(2 * j - 6)
+                st_tr(2 * j - 5)
+            if okg(j - 6):
+                st_osc(j - 6)
+            if j == 3:
+                quant_v(0)
+            if nxt and gl == 3:
+                quant_v(hd + 1)
+            if okg(j - 5):
+                st_qnt(j - 5)
             if nxt:
                 if gl == 1:
                     copy_q(hd + 1)
                 if gl == 2:
                     copy_k(hd + 1)
                     prep_v(hd + 1)
-                if gl == 3:
-                    quant_v(hd + 1)
-            if okg(j - 6):
-                if first_held <= j - 6 and j < last_load:
-                    held.append(j - 6)
+            if okg(j - 7):
+                if first_held <= j - 7 and j < last_load:
+                    held.append(j - 7)
                 else:
-                    store(j - 6)
+                    store(j - 7)
+            if j == 2:
+                prep_v(0)
+            if 1 <= j < H:
+                prior_table(j)
+            if 1 <= j + 1 < H:
+                prior_dist(j + 1)

@@ -27,8 +27,7 @@ FLOPS = 2 * 2 * B * H * S * S * D
 SCALE = 1.0 / math.sqrt(D)
 BIG = 2.0 ** 100
 MASK_BUFS = 5
-OUT_BUFS = 41
-LAST_IN_S = 2
+OUT_BUFS = 44
 
 
 def reach(sigma):
@@ -55,6 +54,7 @@ def tile_gpsdpattention_t_kernel(tc, Q, K, V, attn_mask, out):
         ob = ctx.enter_context(tc.tile_pool(name="ob", bufs=OUT_BUFS))
         wk = ctx.enter_context(tc.tile_pool(name="wk", bufs=4))
         wq = ctx.enter_context(tc.tile_pool(name="wq", bufs=3))
+        wc = ctx.enter_context(tc.tile_pool(name="wc", bufs=5))
         ek = ctx.enter_context(tc.tile_pool(name="ek", bufs=4))
         small = ctx.enter_context(tc.tile_pool(name="small", bufs=8))
         ps_s = ctx.enter_context(tc.psum_pool(name="ps_s", bufs=4))
@@ -207,6 +207,22 @@ def tile_gpsdpattention_t_kernel(tc, Q, K, V, attn_mask, out):
             nc.vector.tensor_reduce(out=negm[:], in_=tl[("sm", g)][:], axis=AX.X, op=ALU.max, negate=True)
             tl[("negm", g)] = negm
 
+        def st_max_tile(n):
+            g, r = divmod(n, R)
+            if r == 0:
+                tl[("negm", g)] = small.tile([P, R], F32, name="negm")
+            nc.vector.tensor_reduce(out=tl[("negm", g)][:, r:r + 1], in_=tl[("sm", g)][:, r, :], axis=AX.X, op=ALU.max,
+                                    negate=True)
+
+        def st_bias_tile(n):
+            g, r = divmod(n, R)
+            if r == 0:
+                tl[("bias", g)] = small.tile([P, R], F32, name="bias")
+                if g % 2 == 0:
+                    tl[("rs2", g // 2)] = gp.tile([P, 2, R], F32, name="rs")
+                tl[("rs", g)] = tl[("rs2", g // 2)][:, g % 2, :]
+            nc.scalar.mul(out=tl[("bias", g)][:, r:r + 1], in_=tl[("negm", g)][:, r:r + 1], mul=SCALE)
+
         def st_bias(g):
             bias = small.tile([P, R], F32, name="bias")
             nc.scalar.mul(out=bias[:], in_=tl[("negm", g)][:], mul=SCALE)
@@ -223,7 +239,7 @@ def tile_gpsdpattention_t_kernel(tc, Q, K, V, attn_mask, out):
             tl[("e", n)] = e
 
         def st_tr(n):
-            if n >= R * (NG - LAST_IN_S):
+            if n >= R * (NG - 2):
                 eT = ps_s.tile([P, 2, 2, P], F32, name="eT", tag="sc")
             else:
                 eT = ps_t.tile([P, 2, 2, P], F32, name="eT", tag="tr")
@@ -233,28 +249,35 @@ def tile_gpsdpattention_t_kernel(tc, Q, K, V, attn_mask, out):
                     nc.tensor.transpose(eT[:, c, u, :], e_w[:, c, u, :], ident_f[:])
             tl[("eT", n)] = eT
 
-        def st_cpy(n):
+        def st_cpy(n, on_vector=False):
             g, r = divmod(n, R)
             if r == 0:
                 tl[("eg", g)] = wq.tile([P, R, 2, P, 4], BF16, name="eg", align_bytes=64)
-            nc.scalar.copy(out=tl[("eg", g)][:, r].bitcast(F32), in_=tl[("eT", n)][:].rearrange("p c u q -> p c q u"))
+            if on_vector:
+                nc.vector.tensor_copy(out=tl[("eg", g)][:, r].bitcast(F32),
+                                      in_=tl[("eT", n)][:].rearrange("p c u q -> p c q u"))
+            else:
+                nc.scalar.copy(out=tl[("eg", g)][:, r].bitcast(F32), in_=tl[("eT", n)][:].rearrange("p c u q -> p c q u"))
 
         def st_qnt(g):
+            ec = wc.tile([P, R * 2 * P], U32, name="ec", align_bytes=64)
+            es = wc.tile([P, R * 2 * P], U8, name="es", align_bytes=64)
+            nc.vector.quantize_mx(out=ec[:].bitcast(FP8X4), scales=es[:],
+                                  in_=tl[("eg", g)][:].rearrange("p r c q t -> p (r c q t)"))
+            tl[("ec", g)] = (ec, es)
             if g % 2 == 0:
                 rinv = gp.tile([P, 2, R], F32, name="rinv")
                 nc.vector.reciprocal(rinv[:], tl[("rs2", g // 2)][:])
                 tl[("rinv", g)] = rinv[:, 0, :]
                 tl[("rinv", g + 1)] = rinv[:, 1, :]
-            ec = wq.tile([P, R * 2 * P], U32, name="ec", align_bytes=64)
-            es = wq.tile([P, R * 2 * P], U8, name="es", align_bytes=64)
-            nc.vector.quantize_mx(out=ec[:].bitcast(FP8X4), scales=es[:],
-                                  in_=tl[("eg", g)][:].rearrange("p r c q t -> p (r c q t)"))
-            tl[("ec", g)] = (ec, es)
 
         def st_mx(g):
             vc, vs = hdt[("v", g // (S // GQ))]
             ec, es = tl[("ec", g)]
-            o_ps = ps_o.tile([P, R, D], F32, name="o_ps")
+            if g in (NG - 3, NG - 2):
+                o_ps = ps_t.tile([P, R, D], F32, name="o_ps", tag="tr")
+            else:
+                o_ps = ps_o.tile([P, R, D], F32, name="o_ps")
             for r in range(R):
                 for c in range(2):
                     ecols = slice((2 * r + c) * P, (2 * r + c + 1) * P)
@@ -286,13 +309,12 @@ def tile_gpsdpattention_t_kernel(tc, Q, K, V, attn_mask, out):
             nc.sync.dma_start(out=o_v[g], in_=tl[("ob", g)][:])
 
         last_load = NG - MASK_BUFS
-        first_held = last_load - 6 - OUT_BUFS + 3
+        first_held = last_load - 5 - OUT_BUFS + 3
         held = []
-        junk_f = const.tile([P, 1], F32, name="junk_f")
-        junk_u = const.tile([P, 1], U32, name="junk_u")
-        for j in range(NG + 8):
+        for j in range(NG):
             hd, gl = divmod(j, GPH)
             nxt = hd + 1 < NH
+            last = j == NG - 1
             if okg(j + MASK_BUFS - 1):
                 load_mask(j + MASK_BUFS - 1, 1)
             if j == last_load:
@@ -300,61 +322,75 @@ def tile_gpsdpattention_t_kernel(tc, Q, K, V, attn_mask, out):
                     store(g)
             if gl == 0 and hd + 2 < NH:
                 load_head(hd + 2)
-            if okg(j - 6):
-                st_mx(j - 6)
+            if okg(j - 5):
+                st_mx(j - 5)
             if nxt and gl == 1:
                 prep_q(hd + 1)
             if nxt and gl == 2:
                 prep_k(hd + 1)
-            if okg(j - 6):
-                nc.gpsimd.tensor_copy(out=junk_u[:], in_=tl[("ec", j - 6)][0][:, 0:1])
-            elif okg(j - 3):
-                nc.gpsimd.tensor_copy(out=junk_f[:], in_=tl[("negm", j - 3)][:, 0:1])
-            if okg(j - 1):
-                st_band(2 * j - 2)
-                st_band(2 * j - 1)
-            if okg(j):
-                st_mask(2 * j)
+            st_mask(2 * j)
+            st_band(2 * j)
             if okg(j + 1):
                 st_qk(2 * j + 2)
-            if okg(j):
-                st_mask(2 * j + 1)
+            st_mask(2 * j + 1)
+            st_band(2 * j + 1)
             if okg(j + 1):
                 st_qk(2 * j + 3)
-            if okg(j - 3):
-                st_bias(j - 3)
-                st_exp(2 * j - 6)
-                st_exp(2 * j - 5)
             if okg(j - 2):
-                st_max(j - 2)
-            if okg(j - 4):
-                st_cpy(2 * j - 8)
-                st_cpy(2 * j - 7)
+                st_bias(j - 2)
+                st_exp(2 * j - 4)
+                st_exp(2 * j - 3)
+            if okg(j - 1) and not last:
+                st_max(j - 1)
             if okg(j - 3):
-                st_tr(2 * j - 6)
-                st_tr(2 * j - 5)
-            if okg(j - 6):
-                st_osc(j - 6)
-            if j == 3:
-                quant_v(0)
-            if nxt and gl == 3:
-                quant_v(hd + 1)
+                st_cpy(2 * j - 6)
+                st_cpy(2 * j - 5)
+            if okg(j - 2):
+                st_tr(2 * j - 4)
+                st_tr(2 * j - 3)
             if okg(j - 5):
-                st_qnt(j - 5)
+                st_osc(j - 5)
+            if okg(j - 4) and not last:
+                st_qnt(j - 4)
             if nxt:
                 if gl == 1:
                     copy_q(hd + 1)
                 if gl == 2:
                     copy_k(hd + 1)
                     prep_v(hd + 1)
-            if okg(j - 7):
-                if first_held <= j - 7 and j < last_load:
-                    held.append(j - 7)
+                if j == 3:
+                    quant_v(0)
+                if gl == 3:
+                    quant_v(hd + 1)
+            if okg(j - 6):
+                if first_held <= j - 6 and j < last_load:
+                    held.append(j - 6)
                 else:
-                    store(j - 7)
+                    store(j - 6)
             if j == 2:
                 prep_v(0)
             if 1 <= j < H:
                 prior_table(j)
             if 1 <= j + 1 < H:
                 prior_dist(j + 1)
+
+        for n in range(R * (NG - 2), R * NG):
+            st_max_tile(n)
+            st_bias_tile(n)
+            st_exp(n)
+            st_tr(n)
+        st_qnt(NG - 5)
+        st_qnt(NG - 4)
+        for g in (NG - 3, NG - 2):
+            st_cpy(R * g, on_vector=True)
+            st_cpy(R * g + 1, on_vector=True)
+            st_qnt(g)
+        st_cpy(R * NG - 2)
+        st_cpy(R * NG - 1)
+        st_qnt(NG - 1)
+        store(NG - 6)
+        for g in range(NG - 5, NG):
+            st_mx(g)
+        for g in range(NG - 5, NG):
+            st_osc(g)
+            store(g)

@@ -39,7 +39,7 @@ def tile_gpsdpattention_t_kernel(tc, Q, K, V, attn_mask, out):
     mask_w = attn_mask.bitcast(I32)
     q_v = Q.rearrange("b h (g p r) d -> (b h) p g r d", p=P, r=R)
     k_v = K.rearrange("b h (p a) d -> (b h) p a d", p=P)
-    v_v = V.rearrange("b h (c p t) d -> (b h) p c t d", p=P, t=4)
+    v_v = V.rearrange("b h (c u p e) d -> (b h) p c u e d", u=2, p=P, e=2)
     m_v = mask_w.rearrange("b h (g p r) w -> (b h g) p r w", p=P, r=R)
     o_v = out.rearrange("b h (g p r) d -> (b h g) p r d", p=P, r=R)
 
@@ -76,8 +76,9 @@ def tile_gpsdpattention_t_kernel(tc, Q, K, V, attn_mask, out):
             raw[("k", hd)] = k_raw
 
         def load_v(hd):
-            v_raw = ld.tile([P, 2, 4, D], BF16, name="v_raw")
-            nc.sync.dma_start(out=v_raw[:], in_=v_v[hd])
+            v_raw = ld.tile([P, 2, 2, 2, D], BF16, name="v_raw")
+            for c in range(2):
+                nc.sync.dma_start(out=v_raw[:, c], in_=v_v[hd, :, c])
             raw[("v", hd)] = v_raw
 
         def load_head(hd):
@@ -161,7 +162,7 @@ def tile_gpsdpattention_t_kernel(tc, Q, K, V, attn_mask, out):
         def prep_v(hd):
             vg = hd_pool.tile([P, 2, D, 4], BF16, name="vg", align_bytes=64)
             for c in range(2):
-                nc.scalar.copy(out=vg[:, c], in_=raw[("v", hd)][:, c].rearrange("p t d -> p d t"))
+                nc.scalar.copy(out=vg[:, c], in_=raw[("v", hd)][:, c].rearrange("p u e d -> p d (u e)"))
             hdt[("vg", hd)] = vg
 
         def quant_v(hd):
@@ -243,7 +244,7 @@ def tile_gpsdpattention_t_kernel(tc, Q, K, V, attn_mask, out):
                 eT = ps_s.tile([P, 2, 2, P], F32, name="eT", tag="sc")
             else:
                 eT = ps_t.tile([P, 2, 2, P], F32, name="eT", tag="tr")
-            e_w = tl[("e", n)][:].bitcast(F32).rearrange("q (c k u) -> q c u k", c=2, u=2)
+            e_w = tl[("e", n)][:].bitcast(F32).rearrange("q (c u k) -> q c u k", c=2, u=2)
             for c in range(2):
                 for u in range(2):
                     nc.tensor.transpose(eT[:, c, u, :], e_w[:, c, u, :], ident_f[:])

import math
from contextlib import ExitStack

import concourse.mybir as mybir
from concourse.masks import make_identity

F32 = mybir.dt.float32
BF16 = mybir.dt.bfloat16
I32 = mybir.dt.int32
U32 = mybir.dt.uint32
U8 = mybir.dt.uint8
FP8X4 = mybir.dt.float8_e4m3fn_x4
ALU = mybir.AluOpType
ACT = mybir.ActivationFunctionType
AX = mybir.AxisListType

B, H, S, D = 4, 4, 1024, 128
P = 128
R = 2
GQ = P * R
NG = B * H * S // GQ
NT = NG * R
NH = B * H
TPH = S // P
SIGMAS = (5.0, 10.0, 20.0, 40.0)
FLOPS = 2 * 2 * B * H * S * S * D
SCALE = 1.0 / math.sqrt(D)
BIG = 2.0 ** 100
MASK_BUFS = 5
OUT_BUFS = 44


def reach(sigma):
    return 4 * ((math.ceil(sigma * math.sqrt(2.0 * math.log(1e12))) + 3) // 4)


def tile_gpsdpattention_t_kernel(tc, Q, K, V, attn_mask, out):
    nc = tc.nc
    mask_w = attn_mask.bitcast(I32)
    q_v = Q.rearrange("b h (g p r) d -> (b h) p g r d", p=P, r=R)
    k_v = K.rearrange("b h (p a) d -> (b h) p a d", p=P)
    v_v = V.rearrange("b h (c u p e) d -> (b h) p c u e d", u=2, p=P, e=2)
    m_v = mask_w.rearrange("b h (g p r) w -> (b h g) p r w", p=P, r=R)
    o_v = out.rearrange("b h (g p r) d -> (b h g) p r d", p=P, r=R)

    with ExitStack() as ctx:
        ctx.enter_context(tc.manual_schedule())
        const = ctx.enter_context(tc.tile_pool(name="const", bufs=1))
        ld = ctx.enter_context(tc.tile_pool(name="ld", bufs=2))
        mk = ctx.enter_context(tc.tile_pool(name="mk", bufs=MASK_BUFS))
        hd_pool = ctx.enter_context(tc.tile_pool(name="hd", bufs=2))
        vq = ctx.enter_context(tc.tile_pool(name="vq", bufs=3))
        gp = ctx.enter_context(tc.tile_pool(name="gp", bufs=4))
        ob = ctx.enter_context(tc.tile_pool(name="ob", bufs=OUT_BUFS))
        wk = ctx.enter_context(tc.tile_pool(name="wk", bufs=4))
        wq = ctx.enter_context(tc.tile_pool(name="wq", bufs=3))
        wc = ctx.enter_context(tc.tile_pool(name="wc", bufs=5))
        ek = ctx.enter_context(tc.tile_pool(name="ek", bufs=4))
        small = ctx.enter_context(tc.tile_pool(name="small", bufs=8))
        ps_s = ctx.enter_context(tc.psum_pool(name="ps_s", bufs=4))
        ps_t = ctx.enter_context(tc.psum_pool(name="ps_t", bufs=2))
        ps_o = ctx.enter_context(tc.psum_pool(name="ps_o", bufs=2))

        raw = {}
        hdt = {}
        tl = {}

        def load_q(hd):
            q_raw = ld.tile([P, S // GQ, R, D], BF16, name="q_raw")
            nc.sync.dma_start(out=q_raw[:], in_=q_v[hd])
            raw[("q", hd)] = q_raw

        def load_k(hd):
            k_raw = ld.tile([P, S // P, D], BF16, name="k_raw")
            nc.sync.dma_start(out=k_raw[:], in_=k_v[hd])
            raw[("k", hd)] = k_raw

        def load_v(hd):
            v_raw = ld.tile([P, 2, 2, 2, D], BF16, name="v_raw")
            for c in range(2):
                nc.sync.dma_start(out=v_raw[:, c], in_=v_v[hd, :, c])
            raw[("v", hd)] = v_raw

        def load_head(hd):
            load_q(hd)
            load_k(hd)
            load_v(hd)

        def load_mask(g, pieces):
            m_raw = mk.tile([P, R, 2 * S], I32, name="m_raw")
            step = R // pieces
            for j in range(pieces):
                nc.sync.dma_start(out=m_raw[:, j * step:(j + 1) * step, :], in_=m_v[g, :, j * step:(j + 1) * step, :])
            tl[("m", g)] = m_raw

        load_k(0)
        load_q(0)
        load_mask(0, R)
        load_mask(1, 1)
        load_q(1)
        load_mask(2, 1)
        load_k(1)
        load_v(0)
        load_mask(3, 1)
        load_v(1)

        warm = const.tile([P, 1], F32, name="warm")
        nc.vector.memset(warm[:], 0.0)
        nc.scalar.activation(out=warm[:], in_=warm[:], func=ACT.Exp)

        ident = const.tile([P, P], BF16, name="ident")
        make_identity(nc, ident[:])

        prior = {}
        pscr = {}

        def prior_dist(h):
            lp = reach(SIGMAS[h])
            wt = GQ + R - 1 + lp
            d_f = const.tile([P, wt], F32, name="d_f", tag="d_f")
            nc.gpsimd.iota(d_f[:], pattern=[[-1, wt]], base=lp + R - 1, channel_multiplier=R,
                           allow_small_or_imprecise_dtypes=True)
            g_t = const.tile([P, wt], F32, name="g_t", tag="g_t")
            nc.scalar.activation(out=g_t[:], in_=d_f[:], func=ACT.Square)
            nc.scalar.activation(out=g_t[:], in_=g_t[:], func=ACT.Exp, scale=-1.0 / (2.0 * SIGMAS[h] ** 2))
            pscr[h] = (d_f, g_t)

        def prior_table(h):
            d_f, g_t = pscr[h]
            nc.gpsimd.tensor_scalar(out=d_f[:], in0=d_f[:], scalar1=0.0, scalar2=math.sqrt(D), op0=ALU.is_ge, op1=ALU.mult)
            tab = const.tile([P, d_f.shape[1]], F32, name="tab%d" % h)
            nc.gpsimd.tensor_tensor(out=tab[:], in0=d_f[:], in1=g_t[:], op=ALU.mult)
            prior[h] = (reach(SIGMAS[h]), tab)

        prior_dist(0)
        prior_table(0)
        ident_f = const.tile([P, P], F32, name="ident_f")
        make_identity(nc, ident_f[:])

        def prep_q(hd):
            qT_ps = ps_o.tile([P, TPH, P], BF16, name="qT_ps", tag="o_ps")
            for t in range(TPH):
                nc.tensor.transpose(qT_ps[:, t, :], raw[("q", hd)][:, t // R, t % R, :], ident[:])
            hdt[("qp", hd)] = qT_ps

        def copy_q(hd):
            qT = hd_pool.tile([P, TPH, P], BF16, name="qT")
            nc.scalar.copy(out=qT[:], in_=hdt[("qp", hd)][:])
            hdt[("q", hd)] = qT

        def prep_k(hd):
            kT_ps = ps_o.tile([P, TPH, P], BF16, name="kT_ps", tag="o_ps")
            for a in range(TPH):
                nc.tensor.transpose(kT_ps[:, a, :], raw[("k", hd)][:, a, :], ident[:])
            hdt[("kp", hd)] = kT_ps

        def copy_k(hd):
            kT = hd_pool.tile([P, P, TPH], BF16, name="kT")
            nc.scalar.copy(out=kT[:], in_=hdt[("kp", hd)][:].rearrange("d a p -> d p a"))
            hdt[("k", hd)] = kT

        def prep_v(hd):
            vg = hd_pool.tile([P, 2, D, 4], BF16, name="vg", align_bytes=64)
            for c in range(2):
                nc.scalar.copy(out=vg[:, c], in_=raw[("v", hd)][:, c].rearrange("p u e d -> p d (u e)"))
            hdt[("vg", hd)] = vg

        def quant_v(hd):
            vc = vq.tile([P, 2 * D], U32, name="vc", align_bytes=64)
            vs = vq.tile([P, 2 * D], U8, name="vs", align_bytes=64)
            nc.vector.quantize_mx(out=vc[:].bitcast(FP8X4), scales=vs[:],
                                  in_=hdt[("vg", hd)][:].rearrange("p c d t -> p (c d t)"))
            hdt[("v", hd)] = (vc, vs)

        def st_qk(n):
            hd, t = divmod(n, TPH)
            kT = hdt[("k", hd)][:].rearrange("d p a -> d (p a)")
            banks = []
            for c in range(2):
                sc = ps_s.tile([P, S // 2], F32, name="sc")
                nc.tensor.matmul(out=sc[:], lhsT=hdt[("q", hd)][:, t, :], rhs=kT[:, c * (S // 2):(c + 1) * (S // 2)],
                                 start=True, stop=True)
                banks.append(sc)
            tl[("sc", n)] = banks

        def st_mask(n):
            g, r = divmod(n, R)
            m_k = tl[("m", g)][:, r, :].rearrange("p (k w) -> p k w", w=2)
            if r == 0:
                tl[("sm", g)] = wk.tile([P, R, S], F32, name="sm")
            for c in range(2):
                cols = slice(c * (S // 2), (c + 1) * (S // 2))
                nc.vector.scalar_tensor_tensor(out=tl[("sm", g)][:, r, cols], in0=m_k[:, cols, 0], scalar=-BIG,
                                               in1=tl[("sc", n)][c][:], op0=ALU.mult, op1=ALU.add)

        def st_band(n):
            g, r = divmod(n, R)
            lp, tab = prior[(g // (S // GQ)) % H]
            sm = tl[("sm", g)]
            j_hi = GQ * (g % (S // GQ)) + GQ
            j_lo = max(0, j_hi - GQ - lp)
            z_hi = GQ + lp + R - 1 - r
            nc.gpsimd.tensor_tensor(out=sm[:, r, j_lo:j_hi], in0=sm[:, r, j_lo:j_hi],
                                    in1=tab[:, z_hi - (j_hi - j_lo):z_hi], op=ALU.add)

        def st_max(g):
            negm = small.tile([P, R], F32, name="negm")
            nc.vector.tensor_reduce(out=negm[:], in_=tl[("sm", g)][:], axis=AX.X, op=ALU.max, negate=True)
            tl[("negm", g)] = negm

        def st_max_tile(n):
            g, r = divmod(n, R)
            if r == 0:
                tl[("negm", g)] = small.tile([P, R], F32, name="negm")
            nc.vector.tensor_reduce(out=tl[("negm", g)][:, r:r + 1], in_=tl[("sm", g)][:, r, :], axis=AX.X, op=ALU.max,
                                    negate=True)

        def st_bias_tile(n):
            g, r = divmod(n, R)
            if r == 0:
                tl[("bias", g)] = small.tile([P, R], F32, name="bias")
                if g % 2 == 0:
                    tl[("rs2", g // 2)] = gp.tile([P, 2, R], F32, name="rs")
                tl[("rs", g)] = tl[("rs2", g // 2)][:, g % 2, :]
            nc.scalar.mul(out=tl[("bias", g)][:, r:r + 1], in_=tl[("negm", g)][:, r:r + 1], mul=SCALE)

        def st_bias(g):
            bias = small.tile([P, R], F32, name="bias")
            nc.scalar.mul(out=bias[:], in_=tl[("negm", g)][:], mul=SCALE)
            tl[("bias", g)] = bias
            if g % 2 == 0:
                tl[("rs2", g // 2)] = gp.tile([P, 2, R], F32, name="rs")
            tl[("rs", g)] = tl[("rs2", g // 2)][:, g % 2, :]

        def st_exp(n):
            g, r = divmod(n, R)
            e = ek.tile([P, S], BF16, name="e")
            nc.scalar.activation(out=e[:], in_=tl[("sm", g)][:, r, :], func=ACT.Exp, bias=tl[("bias", g)][:, r:r + 1],
                                 scale=SCALE, accum_out=tl[("rs", g)][:, r:r + 1])
            tl[("e", n)] = e

        def st_tr(n):
            if n >= R * (NG - 2):
                eT = ps_s.tile([P, 2, 2, P], F32, name="eT", tag="sc")
            else:
                eT = ps_t.tile([P, 2, 2, P], F32, name="eT", tag="tr")
            e_w = tl[("e", n)][:].bitcast(F32).rearrange("q (c u k) -> q c u k", c=2, u=2)
            for c in range(2):
                for u in range(2):
                    nc.tensor.transpose(eT[:, c, u, :], e_w[:, c, u, :], ident_f[:])
            tl[("eT", n)] = eT

        def st_cpy(n, on_vector=False):
            g, r = divmod(n, R)
            if r == 0:
                tl[("eg", g)] = wq.tile([P, R, 2, P, 4], BF16, name="eg", align_bytes=64)
            if on_vector:
                nc.vector.tensor_copy(out=tl[("eg", g)][:, r].bitcast(F32),
                                      in_=tl[("eT", n)][:].rearrange("p c u q -> p c q u"))
            else:
                nc.scalar.copy(out=tl[("eg", g)][:, r].bitcast(F32), in_=tl[("eT", n)][:].rearrange("p c u q -> p c q u"))

        def st_qnt(g):
            ec = wc.tile([P, R * 2 * P], U32, name="ec", align_bytes=64)
            es = wc.tile([P, R * 2 * P], U8, name="es", align_bytes=64)
            nc.vector.quantize_mx(out=ec[:].bitcast(FP8X4), scales=es[:],
                                  in_=tl[("eg", g)][:].rearrange("p r c q t -> p (r c q t)"))
            tl[("ec", g)] = (ec, es)
            if g % 2 == 0:
                rinv = gp.tile([P, 2, R], F32, name="rinv")
                nc.vector.reciprocal(rinv[:], tl[("rs2", g // 2)][:])
                tl[("rinv", g)] = rinv[:, 0, :]
                tl[("rinv", g + 1)] = rinv[:, 1, :]

        def st_mx(g):
            vc, vs = hdt[("v", g // (S // GQ))]
            ec, es = tl[("ec", g)]
            if g in (NG - 3, NG - 2):
                o_ps = ps_t.tile([P, R, D], F32, name="o_ps", tag="tr")
            else:
                o_ps = ps_o.tile([P, R, D], F32, name="o_ps")
            for r in range(R):
                for c in range(2):
                    ecols = slice((2 * r + c) * P, (2 * r + c + 1) * P)
                    vcols = slice(c * P, (c + 1) * P)
                    nc.tensor.matmul_mx(out=o_ps[:, r, :], lhsT=ec[:, ecols].bitcast(FP8X4), lhsT_scale=es[:, ecols],
                                        rhs=vc[:, vcols].bitcast(FP8X4), rhs_scale=vs[:, vcols],
                                        start=(c == 0), stop=(c == 1))
            tl[("o", g)] = o_ps

        def st_osc(g):
            o_sb = ob.tile([P, R, D], F32, name="o_sb")
            for r in range(R):
                nc.scalar.activation(out=o_sb[:, r, :], in_=tl[("o", g)][:, r, :], func=ACT.Copy,
                                     scale=tl[("rinv", g)][:, r:r + 1])
            tl[("ob", g)] = o_sb

        def okg(g):
            return 0 <= g < NG

        prep_k(0)
        copy_k(0)
        prep_q(0)
        copy_q(0)
        st_qk(0)
        st_qk(1)
        GPH = S // GQ

        def store(g):
            nc.sync.dma_start(out=o_v[g], in_=tl[("ob", g)][:])

        last_load = NG - MASK_BUFS
        first_held = last_load - 5 - OUT_BUFS + 3
        held = []
        for j in range(NG):
            hd, gl = divmod(j, GPH)
            nxt = hd + 1 < NH
            last = j == NG - 1
            if okg(j + MASK_BUFS - 1):
                load_mask(j + MASK_BUFS - 1, 1)
            if j == last_load:
                for g in held:
                    store(g)
            if gl == 0 and hd + 2 < NH:
                load_head(hd + 2)
            if okg(j - 5):
                st_mx(j - 5)
            if nxt and gl == 1:
                prep_q(hd + 1)
            if nxt and gl == 2:
                prep_k(hd + 1)
            st_mask(2 * j)
            st_band(2 * j)
            if okg(j + 1):
                st_qk(2 * j + 2)
            st_mask(2 * j + 1)
            st_band(2 * j + 1)
            if okg(j + 1):
                st_qk(2 * j + 3)
            if okg(j - 2):
                st_bias(j - 2)
                st_exp(2 * j - 4)
                st_exp(2 * j - 3)
            if okg(j - 1) and not last:
                st_max(j - 1)
            if okg(j - 3):
                st_cpy(2 * j - 6)
                st_cpy(2 * j - 5)
            if okg(j - 2):
                st_tr(2 * j - 4)
                st_tr(2 * j - 3)
            if okg(j - 5):
                st_osc(j - 5)
            if okg(j - 4) and not last:
                st_qnt(j - 4)
            if nxt:
                if gl == 1:
                    copy_q(hd + 1)
                if gl == 2:
                    copy_k(hd + 1)
                    prep_v(hd + 1)
                if j == 3:
                    quant_v(0)
                if gl == 3:
                    quant_v(hd + 1)
            if okg(j - 6):
                if first_held <= j - 6 and j < last_load:
                    held.append(j - 6)
                else:
                    store(j - 6)
            if j == 2:
                prep_v(0)
            if 1 <= j < H:
                prior_table(j)
            if 1 <= j + 1 < H:
                prior_dist(j + 1)

        for n in range(R * (NG - 2), R * NG):
            st_max_tile(n)
            st_bias_tile(n)
            st_exp(n)
            st_tr(n)
        st_qnt(NG - 5)
        st_qnt(NG - 4)
        for g in (NG - 3, NG - 2):
            st_cpy(R * g, on_vector=True)
            st_cpy(R * g + 1, on_vector=True)
            st_qnt(g)
        st_cpy(R * NG - 2)
        st_cpy(R * NG - 1)
        st_qnt(NG - 1)
        store(NG - 6)
        for g in range(NG - 5, NG):
            st_mx(g)
        for g in range(NG - 5, NG):
            st_osc(g)
            store(g)
